import numpy as np
import ml_dtypes


def mxq(x, axis, fmt="e4m3"):
    dtype, down = {"e4m3": (ml_dtypes.float8_e4m3fn, 7), "e5m2": (ml_dtypes.float8_e5m2, 14)}[fmt]
    v = np.moveaxis(np.asarray(x, np.float32).astype(ml_dtypes.bfloat16).astype(np.float64), axis, -1)
    blocks = v.reshape(v.shape[:-1] + (-1, 32))
    amax = np.abs(blocks).max(-1, keepdims=True)
    byte = np.maximum(np.where(amax > 0, np.frexp(amax)[1] - 1 + 127, 0) - down, 1)
    scale = np.exp2(byte - 127.0)
    codes = (blocks / scale).astype(np.float32).astype(dtype).astype(np.float64)
    return np.moveaxis((codes * scale).reshape(v.shape), -1, axis)


WIDE = False


def mx_kscale(k):
    if not WIDE:
        return np.ones(k)
    levels = np.array([10, -10, 5, -5, 0])
    a = np.random.permutation(np.resize(levels, k // 512 * 4)).reshape(k // 512, 4)
    idx = np.arange(k)
    return np.exp2(a[idx // 512, idx % 128 // 32])


BF16 = ml_dtypes.bfloat16


def bf(x):
    return np.asarray(x, np.float32).astype(BF16)


def f64(x):
    return np.asarray(x).astype(np.float64)


E2M1 = np.array([0.0, 0.5, 1.0, 1.5, 2.0, 3.0, 4.0, 6.0, -0.0, -0.5, -1.0, -1.5, -2.0, -3.0, -4.0, -6.0])


def pack_weight(w, fmt):
    k, n = w.shape
    w = f64(bf(w)).reshape(k // 32, 32, n)
    amax = np.abs(w).max(1)
    if fmt == "e4m3":
        byte = np.frexp(amax)[1] - 1 + 127 - 7
    else:
        mant, ex = np.frexp(amax / 6.0)
        byte = np.where(mant > 0.5, ex, ex - 1) + 127
    byte = np.clip(np.where(amax > 0, byte, 1), 1, 254)
    scaled = (w * np.exp2(127.0 - byte)[:, None, :]).reshape(k, n).astype(np.float32)
    by_word = np.ascontiguousarray(scaled.reshape(k // 512, 128, 4, n).transpose(0, 1, 3, 2))
    if fmt == "e4m3":
        words = by_word.astype(ml_dtypes.float8_e4m3fn).view(np.uint8)
    else:
        c = by_word.astype(ml_dtypes.float4_e2m1fn).view(np.uint8) & 0xF
        words = c[..., 0::2] | (c[..., 1::2] << 4)
    return np.ascontiguousarray(words), np.ascontiguousarray(byte.astype(np.uint8).reshape(k // 512, 16, n))


def unpack_weight(words, scales, fmt):
    g, p, n, _ = words.shape
    if fmt == "e4m3":
        vals = np.ascontiguousarray(words).view(ml_dtypes.float8_e4m3fn).astype(np.float64)
    else:
        nib = np.empty((g, p, n, 4), np.uint8)
        nib[..., 0::2] = words & 0xF
        nib[..., 1::2] = words >> 4
        vals = E2M1[nib]
    vals = vals * np.repeat(np.exp2(scales.astype(np.float64) - 127.0), 8, axis=1)[..., None]
    return vals.transpose(0, 1, 3, 2).reshape(g * 512, n)


B, N, DIM, H, HKV, D, CACHE, WINDOW = 4, 2048, 512, 2, 1, 128, 1536, 1024
EPS = 1e-6
THETA = 10000.0
HALF = D // 2
FMT = "e4m3"


def rms_norm(t, w):
    return t * (1.0 / np.sqrt(np.mean(t * t, axis=-1, keepdims=True) + EPS)) * w


def rope(t, cos, sin):
    t2 = t.reshape(*t.shape[:-1], HALF, 2)
    x0, x1 = t2[..., 0], t2[..., 1]
    c = cos[None, None, :, :]
    s = sin[None, None, :, :]
    r0 = x0 * c - x1 * s
    r1 = x0 * s + x1 * c
    return np.stack([r0, r1], axis=-1).reshape(t.shape)


def setup_inputs():
    s = mx_kscale(DIM)
    ang = np.arange(CACHE, CACHE + N)[:, None] * (1.0 / THETA ** (np.arange(0, D, 2) / D))[None, :]
    x = bf(np.random.standard_normal((B, N, DIM)) * s)
    wq = np.random.standard_normal((H * D, DIM)) / np.sqrt(DIM) / s[None, :]
    wk = np.random.standard_normal((HKV * D, DIM)) / np.sqrt(DIM) / s[None, :]
    wv = np.random.standard_normal((HKV * D, DIM)) / np.sqrt(DIM) / s[None, :]
    Wq_words, Wq_scales = pack_weight(np.ascontiguousarray(wq.T), FMT)
    Wk_words, Wk_scales = pack_weight(np.ascontiguousarray(wk.T), FMT)
    Wv_words, Wv_scales = pack_weight(np.ascontiguousarray(wv.T), FMT)
    return {"x": x,
            "freqs_cos": bf(np.cos(ang)), "freqs_sin": bf(np.sin(ang)),
            "Wq_words": Wq_words, "Wq_scales": Wq_scales,
            "Wk_words": Wk_words, "Wk_scales": Wk_scales,
            "Wv_words": Wv_words, "Wv_scales": Wv_scales,
            "wq_norm": bf(2.0 + 0.2 * np.random.standard_normal(D)),
            "wk_norm": bf(1.0 + 0.1 * np.random.standard_normal(D))}


def reference(x, freqs_cos, freqs_sin, Wq_words, Wq_scales, Wk_words, Wk_scales, Wv_words, Wv_scales, wq_norm, wk_norm):
    xq = mxq(f64(x), 2, "e4m3")
    q = (xq @ unpack_weight(Wq_words, Wq_scales, FMT)).reshape(B, N, H, D).transpose(0, 2, 1, 3)
    k = (xq @ unpack_weight(Wk_words, Wk_scales, FMT)).reshape(B, N, HKV, D).transpose(0, 2, 1, 3)
    v = (xq @ unpack_weight(Wv_words, Wv_scales, FMT)).reshape(B, N, HKV, D).transpose(0, 2, 1, 3)
    q = rms_norm(q, f64(wq_norm))
    k = rms_norm(k, f64(wk_norm))
    q = rope(q, f64(freqs_cos), f64(freqs_sin))
    k = rope(k, f64(freqs_cos), f64(freqs_sin))
    return q, k, v

@@ -1,0 +1,267 @@
+from contextlib import ExitStack
+
+import concourse.mybir as mybir
+from concourse.masks import make_identity
+
+F32 = mybir.dt.float32
+BF16 = mybir.dt.bfloat16
+I32 = mybir.dt.int32
+U32 = mybir.dt.uint32
+U8 = mybir.dt.uint8
+FP8X4 = mybir.dt.float8_e4m3fn_x4
+ACT = mybir.ActivationFunctionType
+ALU = mybir.AluOpType
+
+P = 128
+PACK = 4
+BATCH, TOKENS, DIM = 4, 2048, 512
+HEAD = 128
+HALF = HEAD // 2
+EPS = 1e-6
+ROTATED = 3
+FEATURES = 4 * HEAD
+WORDS = DIM // 2
+
+CHUNK_TILES = 4
+STEP_TILES = 2
+CHUNK_TOKENS = CHUNK_TILES * P
+BLOCKS = TOKENS // CHUNK_TOKENS
+CHUNKS = BATCH * BLOCKS
+STEPS_PER_CHUNK = CHUNK_TILES // STEP_TILES
+STEPS = CHUNKS * STEPS_PER_CHUNK
+SLOTS = TOKENS // P
+
+FLOPS = 2 * BATCH * TOKENS * DIM * FEATURES
+
+
+def tile_slidingcacheattention_pa_t_kernel(
+    tc,
+    x,
+    freqs_cos,
+    freqs_sin,
+    Wq_words,
+    Wq_scales,
+    Wk_words,
+    Wk_scales,
+    Wv_words,
+    Wv_scales,
+    wq_norm,
+    wk_norm,
+    out_0,
+    out_1,
+    out_2,
+):
+    nc = tc.nc
+    with ExitStack() as stack:
+        const = stack.enter_context(tc.tile_pool(name="const", bufs=1))
+        resident = stack.enter_context(tc.tile_pool(name="resident", bufs=CHUNKS))
+        stage = stack.enter_context(tc.tile_pool(name="stage", bufs=3))
+        stats = stack.enter_context(tc.tile_pool(name="stats", bufs=4))
+        results = stack.enter_context(tc.tile_pool(name="results", bufs=3))
+        flipped_pool = stack.enter_context(tc.psum_pool(name="flipped_pool", bufs=2))
+        proj_pool = stack.enter_context(tc.psum_pool(name="proj_pool", bufs=3 * STEP_TILES))
+        stack.enter_context(tc.manual_schedule())
+
+        def chunk_rows(chunk):
+            block = chunk % BLOCKS
+            return chunk // BLOCKS, slice(block * CHUNK_TOKENS, (block + 1) * CHUNK_TOKENS)
+
+        x_chunks = []
+
+        def load_x(chunk):
+            b, rows = chunk_rows(chunk)
+            x_chunk = resident.tile([P, CHUNK_TILES, DIM], BF16)
+            nc.sync.dma_start(
+                out=x_chunk[:], in_=x[b, rows, :].rearrange("(p t) k -> p t k", t=CHUNK_TILES)
+            )
+            x_chunks.append(x_chunk)
+
+        load_x(0)
+
+        angle = const.tile([P, 3, SLOTS, HALF], BF16)
+        for plane, freqs in enumerate((freqs_cos, freqs_sin, freqs_cos)):
+            nc.sync.dma_start(
+                out=angle[:, plane].rearrange("p (c t) i -> p c (t i)", t=CHUNK_TILES),
+                in_=freqs.rearrange("(c p t) i -> p c (t i)", p=P, t=CHUNK_TILES),
+            )
+        norm_gain = const.tile([P, 2, HEAD], BF16)
+        nc.sync.dma_start(out=norm_gain[:, 0, :], in_=wq_norm.partition_broadcast(P))
+        nc.sync.dma_start(out=norm_gain[:, 1, :], in_=wk_norm.partition_broadcast(P))
+
+        weights = (
+            (Wq_words, Wq_scales, 0, 2 * HEAD),
+            (Wk_words, Wk_scales, 2 * HEAD, HEAD),
+            (Wv_words, Wv_scales, 3 * HEAD, HEAD),
+        )
+        w_codes = const.tile([P, FEATURES], U32, align_bytes=64)
+        for words, scales, first, width in weights:
+            nc.sync.dma_start(
+                out=w_codes[:, first : first + width].bitcast(I32),
+                in_=words.rearrange("g p n t -> (g p) (n t)").bitcast(I32),
+            )
+        w_scales = const.tile([P, FEATURES], U8, align_bytes=64)
+        nc.vector.memset(w_scales[:].bitcast(I32), 0)
+        for words, scales, first, width in weights:
+            for quadrant in range(4):
+                nc.sync.dma_start(
+                    out=w_scales[32 * quadrant : 32 * quadrant + 4, first : first + width].bitcast(I32),
+                    in_=scales[0, 4 * quadrant : 4 * quadrant + 4, :].bitcast(I32),
+                )
+        for chunk in range(1, CHUNKS):
+            load_x(chunk)
+
+        identity = const.tile([P, P], F32)
+        make_identity(nc, identity[:])
+        eps = const.tile([P, 1], F32)
+        nc.vector.memset(eps[:], EPS)
+        warm = const.tile([P, 1], F32)
+        nc.scalar.activation(out=warm[:], in_=eps[:], func=ACT.Sqrt)
+
+        gain_pairs = norm_gain[:].rearrange("p kind (i two) -> p kind i two", two=2)
+        gain_even = const.tile([P, 2, HALF, 2], F32)
+        gain_odd = const.tile([P, 2, HALF, 2], F32)
+        nc.vector.tensor_copy(out=gain_even[:], in_=gain_pairs[:, :, :, 0:1].to_broadcast([P, 2, HALF, 2]))
+        nc.vector.tensor_scalar_mul(out=gain_odd[:, :, :, 0:1], in0=gain_pairs[:, :, :, 1:2], scalar1=-1.0)
+        nc.vector.tensor_copy(out=gain_odd[:, :, :, 1:2], in_=gain_pairs[:, :, :, 1:2])
+        gains = (gain_even, gain_odd)
+
+        tables = [
+            [const.tile([P, SLOTS, HEAD], F32, name="table_%d_%d" % (kind, parity)) for parity in range(2)]
+            for kind in range(2)
+        ]
+
+        def build_tables(block):
+            slots = slice(block * CHUNK_TILES, (block + 1) * CHUNK_TILES)
+            for kind in range(2):
+                for parity in range(2):
+                    nc.vector.tensor_tensor(
+                        out=tables[kind][parity][:, slots, :].rearrange("p s (i two) -> p s i two", two=2),
+                        in0=angle[:, parity : parity + 2, slots, :].rearrange("p two s i -> p s i two"),
+                        in1=gains[parity][:, kind].unsqueeze(1).to_broadcast([P, CHUNK_TILES, HALF, 2]),
+                        op=ALU.mult,
+                    )
+
+        flipped_of, grouped_of, proj_of, rms_of, values_of = {}, {}, {}, {}, {}
+
+        def tiles_of(step):
+            first = (step % STEPS_PER_CHUNK) * STEP_TILES
+            return step // STEPS_PER_CHUNK, range(first, first + STEP_TILES)
+
+        def transpose(step):
+            chunk, tiles = tiles_of(step)
+            flipped = flipped_pool.tile([P, STEP_TILES, 2, P], F32)
+            for a, t in enumerate(tiles):
+                words = x_chunks[chunk][:, t, :].bitcast(F32)
+                for u in range(2):
+                    nc.tensor.transpose(flipped[:, a, u, :], words[:, u:WORDS:2], identity[:])
+            flipped_of[step] = flipped
+
+        def regroup(step):
+            grouped = stage.tile([P, STEP_TILES, P, PACK], BF16, align_bytes=64)
+            nc.scalar.copy(out=grouped[:].bitcast(F32), in_=flipped_of[step][:].rearrange("p a u r -> p a r u"))
+            grouped_of[step] = grouped
+
+        def project(step):
+            x_codes = stage.tile([P, STEP_TILES * P], U32, align_bytes=64)
+            x_scales = stage.tile([P, STEP_TILES * P], U8, align_bytes=64)
+            nc.vector.quantize_mx(
+                out=x_codes[:].bitcast(FP8X4),
+                scales=x_scales[:],
+                in_=grouped_of[step][:].rearrange("p a r j -> p (a r j)"),
+            )
+            proj_of[step] = []
+            for a in range(STEP_TILES):
+                tokens = slice(a * P, (a + 1) * P)
+                proj = proj_pool.tile([P, FEATURES], F32)
+                nc.tensor.matmul_mx(
+                    out=proj[:],
+                    lhsT=x_codes[:, tokens].bitcast(FP8X4),
+                    lhsT_scale=x_scales[:, tokens],
+                    rhs=w_codes[:].bitcast(FP8X4),
+                    rhs_scale=w_scales[:],
+                    start=True,
+                    stop=True,
+                )
+                proj_of[step].append(proj)
+
+        def norm(step):
+            chunk, tiles = tiles_of(step)
+            if step % STEPS_PER_CHUNK == 0:
+                values = results.tile([P, CHUNK_TILES, HEAD], F32)
+                values_of[chunk] = values
+            squares = stage.tile([P, STEP_TILES, ROTATED, HEAD], BF16)
+            sumsq = stats.tile([P, STEP_TILES * ROTATED], F32)
+            for a, t in enumerate(tiles):
+                proj = proj_of[step][a]
+                for h in range(ROTATED):
+                    nc.scalar.activation(
+                        out=squares[:, a, h, :],
+                        in_=proj[:, h * HEAD : (h + 1) * HEAD],
+                        func=ACT.Square,
+                        accum_out=sumsq[:, a * ROTATED + h : a * ROTATED + h + 1],
+                    )
+                nc.scalar.copy(out=values_of[chunk][:, t, :], in_=proj[:, ROTATED * HEAD : FEATURES])
+            rms = stats.tile([P, STEP_TILES * ROTATED], F32)
+            nc.scalar.activation(out=rms[:], in_=sumsq[:], func=ACT.Sqrt, scale=1.0 / HEAD, bias=eps[:])
+            rms_of[step] = rms
+
+        rotated_of = {}
+
+        def rotate(step):
+            chunk, tiles = tiles_of(step)
+            block = chunk % BLOCKS
+            if step % STEPS_PER_CHUNK == 0:
+                rotated = results.tile([P, ROTATED, CHUNK_TILES, HEAD], F32)
+                rotated_of[chunk] = rotated
+            first = stage.tile([P, ROTATED, STEP_TILES, HEAD], F32)
+            second = stage.tile([P, ROTATED, STEP_TILES, HEAD], F32)
+            rstd = stats.tile([P, STEP_TILES * ROTATED], F32)
+            nc.vector.reciprocal(out=rstd[:], in_=rms_of[step][:])
+            for a, t in enumerate(tiles):
+                for h in range(ROTATED):
+                    kind = h // 2
+                    pairs = proj_of[step][a][:, h * HEAD : (h + 1) * HEAD].rearrange("p (i two) -> p i two", two=2)
+                    for parity, product in enumerate((first[:, h, a, :], second[:, h, a, :])):
+                        nc.vector.scalar_tensor_tensor(
+                            out=product.rearrange("p (i two) -> p i two", two=2),
+                            in0=pairs[:, :, parity : parity + 1].to_broadcast([P, HALF, 2]),
+                            scalar=rstd[:, a * ROTATED + h : a * ROTATED + h + 1],
+                            in1=tables[kind][parity][:, block * CHUNK_TILES + t, :].rearrange("p (i two) -> p i two", two=2),
+                            op0=ALU.mult,
+                            op1=ALU.mult,
+                        )
+            nc.gpsimd.tensor_tensor(
+                out=rotated_of[chunk][:, :, tiles[0] : tiles[0] + STEP_TILES, :], in0=first[:], in1=second[:], op=ALU.add
+            )
+
+        def store(chunk):
+            b, rows = chunk_rows(chunk)
+            nc.sync.dma_start(
+                out=out_0[b, :, rows, :].rearrange("h (p t) d -> p h (t d)", t=CHUNK_TILES),
+                in_=rotated_of[chunk][:, 0:2].rearrange("p h t d -> p h (t d)"),
+            )
+            nc.sync.dma_start(
+                out=out_1[b, 0, rows, :].rearrange("(p t) d -> p (t d)", t=CHUNK_TILES),
+                in_=rotated_of[chunk][:, 2].rearrange("p t d -> p (t d)"),
+            )
+            nc.sync.dma_start(
+                out=out_2[b, 0, rows, :].rearrange("(p t) d -> p (t d)", t=CHUNK_TILES),
+                in_=values_of[chunk][:].rearrange("p t d -> p (t d)"),
+            )
+
+        LEAD = 3
+        for step in range(-LEAD, STEPS):
+            if step + LEAD < BLOCKS:
+                build_tables(step + LEAD)
+            if step + 3 < STEPS:
+                transpose(step + 3)
+            if 0 <= step + 2 < STEPS:
+                project(step + 2)
+            if 0 <= step + 1 < STEPS:
+                norm(step + 1)
+            if step + 3 < STEPS:
+                regroup(step + 3)
+            if step >= 0:
+                rotate(step)
+                if step % STEPS_PER_CHUNK == STEPS_PER_CHUNK - 1:
+                    store(step // STEPS_PER_CHUNK)

@@ -24,11 +24,11 @@ WORDS = DIM // 2
 
 CHUNK_TILES = 4
 STEP_TILES = 2
+CHUNK_STEPS = CHUNK_TILES // STEP_TILES
 CHUNK_TOKENS = CHUNK_TILES * P
 BLOCKS = TOKENS // CHUNK_TOKENS
 CHUNKS = BATCH * BLOCKS
-STEPS_PER_CHUNK = CHUNK_TILES // STEP_TILES
-STEPS = CHUNKS * STEPS_PER_CHUNK
+STEPS = CHUNKS * CHUNK_STEPS
 SLOTS = TOKENS // P
 
 FLOPS = 2 * BATCH * TOKENS * DIM * FEATURES
@@ -57,7 +57,6 @@ def tile_slidingcacheattention_pa_t_kernel(
         resident = stack.enter_context(tc.tile_pool(name="resident", bufs=CHUNKS))
         stage = stack.enter_context(tc.tile_pool(name="stage", bufs=3))
         stats = stack.enter_context(tc.tile_pool(name="stats", bufs=4))
-        results = stack.enter_context(tc.tile_pool(name="results", bufs=3))
         flipped_pool = stack.enter_context(tc.psum_pool(name="flipped_pool", bufs=2))
         proj_pool = stack.enter_context(tc.psum_pool(name="proj_pool", bufs=3 * STEP_TILES))
         stack.enter_context(tc.manual_schedule())
@@ -78,8 +77,8 @@ def tile_slidingcacheattention_pa_t_kernel(
 
         load_x(0)
 
-        angle = const.tile([P, 3, SLOTS, HALF], BF16)
-        for plane, freqs in enumerate((freqs_cos, freqs_sin, freqs_cos)):
+        angle = const.tile([P, 4, SLOTS, HALF], BF16)
+        for plane, freqs in enumerate((freqs_cos, freqs_sin)):
             nc.sync.dma_start(
                 out=angle[:, plane].rearrange("p (c t) i -> p c (t i)", t=CHUNK_TILES),
                 in_=freqs.rearrange("(c p t) i -> p c (t i)", p=P, t=CHUNK_TILES),
@@ -99,6 +98,7 @@ def tile_slidingcacheattention_pa_t_kernel(
                 out=w_codes[:, first : first + width].bitcast(I32),
                 in_=words.rearrange("g p n t -> (g p) (n t)").bitcast(I32),
             )
+        load_x(1)
         w_scales = const.tile([P, FEATURES], U8, align_bytes=64)
         nc.vector.memset(w_scales[:].bitcast(I32), 0)
         for words, scales, first, width in weights:
@@ -107,7 +107,7 @@ def tile_slidingcacheattention_pa_t_kernel(
                     out=w_scales[32 * quadrant : 32 * quadrant + 4, first : first + width].bitcast(I32),
                     in_=scales[0, 4 * quadrant : 4 * quadrant + 4, :].bitcast(I32),
                 )
-        for chunk in range(1, CHUNKS):
+        for chunk in range(2, CHUNKS):
             load_x(chunk)
 
         identity = const.tile([P, P], F32)
@@ -117,35 +117,33 @@ def tile_slidingcacheattention_pa_t_kernel(
         warm = const.tile([P, 1], F32)
         nc.scalar.activation(out=warm[:], in_=eps[:], func=ACT.Sqrt)
 
+        nc.vector.tensor_copy(out=angle[:, 2], in_=angle[:, 1])
+        nc.vector.tensor_copy(out=angle[:, 3], in_=angle[:, 0])
         gain_pairs = norm_gain[:].rearrange("p kind (i two) -> p kind i two", two=2)
-        gain_even = const.tile([P, 2, HALF, 2], F32)
-        gain_odd = const.tile([P, 2, HALF, 2], F32)
-        nc.vector.tensor_copy(out=gain_even[:], in_=gain_pairs[:, :, :, 0:1].to_broadcast([P, 2, HALF, 2]))
-        nc.vector.tensor_scalar_mul(out=gain_odd[:, :, :, 0:1], in0=gain_pairs[:, :, :, 1:2], scalar1=-1.0)
-        nc.vector.tensor_copy(out=gain_odd[:, :, :, 1:2], in_=gain_pairs[:, :, :, 1:2])
-        gains = (gain_even, gain_odd)
+        gains = const.tile([P, 2, HALF, 4], F32)
+        nc.vector.tensor_copy(out=gains[:, :, :, 0:2], in_=gain_pairs[:, :, :, 0:1].to_broadcast([P, 2, HALF, 2]))
+        nc.vector.tensor_scalar_mul(out=gains[:, :, :, 2:3], in0=gain_pairs[:, :, :, 1:2], scalar1=-1.0)
+        nc.vector.tensor_copy(out=gains[:, :, :, 3:4], in_=gain_pairs[:, :, :, 1:2])
 
-        tables = [
-            [const.tile([P, SLOTS, HEAD], F32, name="table_%d_%d" % (kind, parity)) for parity in range(2)]
-            for kind in range(2)
-        ]
+        tables = [const.tile([P, SLOTS, 2 * HEAD], F32, name="table_%d" % kind) for kind in range(2)]
 
         def build_tables(block):
+            builder = nc.vector if block < BLOCKS // 2 else nc.gpsimd
             slots = slice(block * CHUNK_TILES, (block + 1) * CHUNK_TILES)
             for kind in range(2):
-                for parity in range(2):
-                    nc.vector.tensor_tensor(
-                        out=tables[kind][parity][:, slots, :].rearrange("p s (i two) -> p s i two", two=2),
-                        in0=angle[:, parity : parity + 2, slots, :].rearrange("p two s i -> p s i two"),
-                        in1=gains[parity][:, kind].unsqueeze(1).to_broadcast([P, CHUNK_TILES, HALF, 2]),
-                        op=ALU.mult,
-                    )
+                builder.tensor_tensor(
+                    out=tables[kind][:, slots, :].rearrange("p s (i f) -> p s i f", f=4),
+                    in0=angle[:, :, slots, :].rearrange("p f s i -> p s i f"),
+                    in1=gains[:, kind].unsqueeze(1).to_broadcast([P, CHUNK_TILES, HALF, 4]),
+                    op=ALU.mult,
+                )
 
-        flipped_of, grouped_of, proj_of, rms_of, values_of = {}, {}, {}, {}, {}
+        flipped_of, grouped_of, quantised_of, proj_of, rms_of = {}, {}, {}, {}, {}
+        values_of, products_of = {}, {}
 
         def tiles_of(step):
-            first = (step % STEPS_PER_CHUNK) * STEP_TILES
-            return step // STEPS_PER_CHUNK, range(first, first + STEP_TILES)
+            first = (step % CHUNK_STEPS) * STEP_TILES
+            return step // CHUNK_STEPS, range(first, first + STEP_TILES)
 
         def transpose(step):
             chunk, tiles = tiles_of(step)
@@ -157,21 +155,31 @@ def tile_slidingcacheattention_pa_t_kernel(
             flipped_of[step] = flipped
 
         def regroup(step):
-            grouped = stage.tile([P, STEP_TILES, P, PACK], BF16, align_bytes=64)
-            nc.scalar.copy(out=grouped[:].bitcast(F32), in_=flipped_of[step][:].rearrange("p a u r -> p a r u"))
-            grouped_of[step] = grouped
+            chunk, tiles = tiles_of(step)
+            if step % CHUNK_STEPS == 0:
+                grouped = stage.tile([P, CHUNK_TILES, P, PACK], BF16, align_bytes=64)
+                grouped_of[chunk] = grouped
+            nc.scalar.copy(
+                out=grouped_of[chunk][:, tiles[0] : tiles[0] + STEP_TILES].bitcast(F32),
+                in_=flipped_of[step][:].rearrange("p a u r -> p a r u"),
+            )
 
-        def project(step):
-            x_codes = stage.tile([P, STEP_TILES * P], U32, align_bytes=64)
-            x_scales = stage.tile([P, STEP_TILES * P], U8, align_bytes=64)
+        def quantise(chunk):
+            x_codes = stage.tile([P, CHUNK_TOKENS], U32, align_bytes=64)
+            x_scales = stage.tile([P, CHUNK_TOKENS], U8, align_bytes=64)
             nc.vector.quantize_mx(
                 out=x_codes[:].bitcast(FP8X4),
                 scales=x_scales[:],
-                in_=grouped_of[step][:].rearrange("p a r j -> p (a r j)"),
+                in_=grouped_of[chunk][:].rearrange("p t r j -> p (t r j)"),
             )
+            quantised_of[chunk] = (x_codes, x_scales)
+
+        def project(step):
+            chunk, tiles = tiles_of(step)
+            x_codes, x_scales = quantised_of[chunk]
             proj_of[step] = []
-            for a in range(STEP_TILES):
-                tokens = slice(a * P, (a + 1) * P)
+            for t in tiles:
+                tokens = slice(t * P, (t + 1) * P)
                 proj = proj_pool.tile([P, FEATURES], F32)
                 nc.tensor.matmul_mx(
                     out=proj[:],
@@ -186,8 +194,8 @@ def tile_slidingcacheattention_pa_t_kernel(
 
         def norm(step):
             chunk, tiles = tiles_of(step)
-            if step % STEPS_PER_CHUNK == 0:
-                values = results.tile([P, CHUNK_TILES, HEAD], F32)
+            if step % CHUNK_STEPS == 0:
+                values = stage.tile([P, CHUNK_TILES, HEAD], F32)
                 values_of[chunk] = values
             squares = stage.tile([P, STEP_TILES, ROTATED, HEAD], BF16)
             sumsq = stats.tile([P, STEP_TILES * ROTATED], F32)
@@ -205,63 +213,63 @@ def tile_slidingcacheattention_pa_t_kernel(
             nc.scalar.activation(out=rms[:], in_=sumsq[:], func=ACT.Sqrt, scale=1.0 / HEAD, bias=eps[:])
             rms_of[step] = rms
 
-        rotated_of = {}
-
         def rotate(step):
             chunk, tiles = tiles_of(step)
             block = chunk % BLOCKS
-            if step % STEPS_PER_CHUNK == 0:
-                rotated = results.tile([P, ROTATED, CHUNK_TILES, HEAD], F32)
-                rotated_of[chunk] = rotated
-            first = stage.tile([P, ROTATED, STEP_TILES, HEAD], F32)
-            second = stage.tile([P, ROTATED, STEP_TILES, HEAD], F32)
+            if step % CHUNK_STEPS == 0:
+                products = stage.tile([P, ROTATED, CHUNK_TILES, 2 * HEAD], F32)
+                products_of[chunk] = products
             rstd = stats.tile([P, STEP_TILES * ROTATED], F32)
             nc.vector.reciprocal(out=rstd[:], in_=rms_of[step][:])
             for a, t in enumerate(tiles):
                 for h in range(ROTATED):
                     kind = h // 2
-                    pairs = proj_of[step][a][:, h * HEAD : (h + 1) * HEAD].rearrange("p (i two) -> p i two", two=2)
-                    for parity, product in enumerate((first[:, h, a, :], second[:, h, a, :])):
-                        nc.vector.scalar_tensor_tensor(
-                            out=product.rearrange("p (i two) -> p i two", two=2),
-                            in0=pairs[:, :, parity : parity + 1].to_broadcast([P, HALF, 2]),
-                            scalar=rstd[:, a * ROTATED + h : a * ROTATED + h + 1],
-                            in1=tables[kind][parity][:, block * CHUNK_TILES + t, :].rearrange("p (i two) -> p i two", two=2),
-                            op0=ALU.mult,
-                            op1=ALU.mult,
-                        )
-            nc.gpsimd.tensor_tensor(
-                out=rotated_of[chunk][:, :, tiles[0] : tiles[0] + STEP_TILES, :], in0=first[:], in1=second[:], op=ALU.add
-            )
+                    nc.vector.scalar_tensor_tensor(
+                        out=products_of[chunk][:, h, t, :].rearrange("p (d two) -> p d two", two=2),
+                        in0=proj_of[step][a][:, h * HEAD : (h + 1) * HEAD].unsqueeze(2).to_broadcast([P, HEAD, 2]),
+                        scalar=rstd[:, a * ROTATED + h : a * ROTATED + h + 1],
+                        in1=tables[kind][:, block * CHUNK_TILES + t, :].rearrange("p (d two) -> p d two", two=2),
+                        op0=ALU.mult,
+                        op1=ALU.mult,
+                    )
 
-        def store(chunk):
+        def finish(chunk):
             b, rows = chunk_rows(chunk)
+            by_pair = products_of[chunk][:].rearrange("p h t (i y two) -> p (h t i) y two", y=2, two=2)
+            rotated = stage.tile([P, ROTATED, CHUNK_TILES, HEAD], F32)
+            nc.gpsimd.tensor_tensor(
+                out=rotated[:].rearrange("p h t (i two) -> p (h t i) two", two=2),
+                in0=by_pair[:, :, 0, :],
+                in1=by_pair[:, :, 1, :],
+                op=ALU.add,
+            )
             nc.sync.dma_start(
                 out=out_0[b, :, rows, :].rearrange("h (p t) d -> p h (t d)", t=CHUNK_TILES),
-                in_=rotated_of[chunk][:, 0:2].rearrange("p h t d -> p h (t d)"),
+                in_=rotated[:, 0:2].rearrange("p h t d -> p h (t d)"),
             )
             nc.sync.dma_start(
                 out=out_1[b, 0, rows, :].rearrange("(p t) d -> p (t d)", t=CHUNK_TILES),
-                in_=rotated_of[chunk][:, 2].rearrange("p t d -> p (t d)"),
+                in_=rotated[:, 2].rearrange("p t d -> p (t d)"),
             )
             nc.sync.dma_start(
                 out=out_2[b, 0, rows, :].rearrange("(p t) d -> p (t d)", t=CHUNK_TILES),
                 in_=values_of[chunk][:].rearrange("p t d -> p (t d)"),
             )
 
-        LEAD = 3
-        for step in range(-LEAD, STEPS):
-            if step + LEAD < BLOCKS:
-                build_tables(step + LEAD)
-            if step + 3 < STEPS:
-                transpose(step + 3)
+        for step in range(-4, STEPS):
+            if step + 4 < STEPS:
+                transpose(step + 4)
             if 0 <= step + 2 < STEPS:
+                if (step + 2) % CHUNK_STEPS == 0:
+                    quantise((step + 2) // CHUNK_STEPS)
                 project(step + 2)
+            if (step + 4) % CHUNK_STEPS == 0 and (step + 4) // CHUNK_STEPS < BLOCKS:
+                build_tables((step + 4) // CHUNK_STEPS)
             if 0 <= step + 1 < STEPS:
                 norm(step + 1)
-            if step + 3 < STEPS:
-                regroup(step + 3)
+            if step + 4 < STEPS:
+                regroup(step + 4)
             if step >= 0:
                 rotate(step)
-                if step % STEPS_PER_CHUNK == STEPS_PER_CHUNK - 1:
-                    store(step // STEPS_PER_CHUNK)
+                if step % CHUNK_STEPS == CHUNK_STEPS - 1:
+                    finish(step // CHUNK_STEPS)

@@ -24,11 +24,11 @@ WORDS = DIM // 2
 
 CHUNK_TILES = 4
 STEP_TILES = 2
-CHUNK_STEPS = CHUNK_TILES // STEP_TILES
 CHUNK_TOKENS = CHUNK_TILES * P
 BLOCKS = TOKENS // CHUNK_TOKENS
 CHUNKS = BATCH * BLOCKS
-STEPS = CHUNKS * CHUNK_STEPS
+STEPS_PER_CHUNK = CHUNK_TILES // STEP_TILES
+STEPS = CHUNKS * STEPS_PER_CHUNK
 SLOTS = TOKENS // P
 
 FLOPS = 2 * BATCH * TOKENS * DIM * FEATURES
@@ -57,6 +57,7 @@ def tile_slidingcacheattention_pa_t_kernel(
         resident = stack.enter_context(tc.tile_pool(name="resident", bufs=CHUNKS))
         stage = stack.enter_context(tc.tile_pool(name="stage", bufs=3))
         stats = stack.enter_context(tc.tile_pool(name="stats", bufs=4))
+        results = stack.enter_context(tc.tile_pool(name="results", bufs=3))
         flipped_pool = stack.enter_context(tc.psum_pool(name="flipped_pool", bufs=2))
         proj_pool = stack.enter_context(tc.psum_pool(name="proj_pool", bufs=3 * STEP_TILES))
         stack.enter_context(tc.manual_schedule())
@@ -77,8 +78,8 @@ def tile_slidingcacheattention_pa_t_kernel(
 
         load_x(0)
 
-        angle = const.tile([P, 4, SLOTS, HALF], BF16)
-        for plane, freqs in enumerate((freqs_cos, freqs_sin)):
+        angle = const.tile([P, 3, SLOTS, HALF], BF16)
+        for plane, freqs in enumerate((freqs_cos, freqs_sin, freqs_cos)):
             nc.sync.dma_start(
                 out=angle[:, plane].rearrange("p (c t) i -> p c (t i)", t=CHUNK_TILES),
                 in_=freqs.rearrange("(c p t) i -> p c (t i)", p=P, t=CHUNK_TILES),
@@ -98,7 +99,6 @@ def tile_slidingcacheattention_pa_t_kernel(
                 out=w_codes[:, first : first + width].bitcast(I32),
                 in_=words.rearrange("g p n t -> (g p) (n t)").bitcast(I32),
             )
-        load_x(1)
         w_scales = const.tile([P, FEATURES], U8, align_bytes=64)
         nc.vector.memset(w_scales[:].bitcast(I32), 0)
         for words, scales, first, width in weights:
@@ -107,7 +107,7 @@ def tile_slidingcacheattention_pa_t_kernel(
                     out=w_scales[32 * quadrant : 32 * quadrant + 4, first : first + width].bitcast(I32),
                     in_=scales[0, 4 * quadrant : 4 * quadrant + 4, :].bitcast(I32),
                 )
-        for chunk in range(2, CHUNKS):
+        for chunk in range(1, CHUNKS):
             load_x(chunk)
 
         identity = const.tile([P, P], F32)
@@ -115,35 +115,37 @@ def tile_slidingcacheattention_pa_t_kernel(
         eps = const.tile([P, 1], F32)
         nc.vector.memset(eps[:], EPS)
         warm = const.tile([P, 1], F32)
-        nc.scalar.activation(out=warm[:], in_=eps[:], func=ACT.Sqrt)
+        nc.scalar.activation(out=warm[:], in_=eps[:], func=ACT.Abs_reciprocal_sqrt)
 
-        nc.vector.tensor_copy(out=angle[:, 2], in_=angle[:, 1])
-        nc.vector.tensor_copy(out=angle[:, 3], in_=angle[:, 0])
         gain_pairs = norm_gain[:].rearrange("p kind (i two) -> p kind i two", two=2)
-        gains = const.tile([P, 2, HALF, 4], F32)
-        nc.vector.tensor_copy(out=gains[:, :, :, 0:2], in_=gain_pairs[:, :, :, 0:1].to_broadcast([P, 2, HALF, 2]))
-        nc.vector.tensor_scalar_mul(out=gains[:, :, :, 2:3], in0=gain_pairs[:, :, :, 1:2], scalar1=-1.0)
-        nc.vector.tensor_copy(out=gains[:, :, :, 3:4], in_=gain_pairs[:, :, :, 1:2])
+        gain_even = const.tile([P, 2, HALF, 2], F32)
+        gain_odd = const.tile([P, 2, HALF, 2], F32)
+        nc.vector.tensor_copy(out=gain_even[:], in_=gain_pairs[:, :, :, 0:1].to_broadcast([P, 2, HALF, 2]))
+        nc.vector.tensor_scalar_mul(out=gain_odd[:, :, :, 0:1], in0=gain_pairs[:, :, :, 1:2], scalar1=-1.0)
+        nc.vector.tensor_copy(out=gain_odd[:, :, :, 1:2], in_=gain_pairs[:, :, :, 1:2])
+        gains = (gain_even, gain_odd)
 
-        tables = [const.tile([P, SLOTS, 2 * HEAD], F32, name="table_%d" % kind) for kind in range(2)]
+        tables = [
+            [const.tile([P, SLOTS, HEAD], F32, name="table_%d_%d" % (kind, parity)) for parity in range(2)]
+            for kind in range(2)
+        ]
 
         def build_tables(block):
-            builder = nc.vector if block < BLOCKS // 2 else nc.gpsimd
             slots = slice(block * CHUNK_TILES, (block + 1) * CHUNK_TILES)
             for kind in range(2):
-                builder.tensor_tensor(
-                    out=tables[kind][:, slots, :].rearrange("p s (i f) -> p s i f", f=4),
-                    in0=angle[:, :, slots, :].rearrange("p f s i -> p s i f"),
-                    in1=gains[:, kind].unsqueeze(1).to_broadcast([P, CHUNK_TILES, HALF, 4]),
-                    op=ALU.mult,
-                )
+                for parity in range(2):
+                    nc.vector.tensor_tensor(
+                        out=tables[kind][parity][:, slots, :].rearrange("p s (i two) -> p s i two", two=2),
+                        in0=angle[:, parity : parity + 2, slots, :].rearrange("p two s i -> p s i two"),
+                        in1=gains[parity][:, kind].unsqueeze(1).to_broadcast([P, CHUNK_TILES, HALF, 2]),
+                        op=ALU.mult,
+                    )
 
-        flipped_of, grouped_of, quantised_of, proj_of, rms_of = {}, {}, {}, {}, {}
-        values_of, products_of = {}, {}
+        flipped_of, grouped_of, proj_of, rstd_of, values_of = {}, {}, {}, {}, {}
 
         def tiles_of(step):
-            first = (step % CHUNK_STEPS) * STEP_TILES
-            return step // CHUNK_STEPS, range(first, first + STEP_TILES)
+            first = (step % STEPS_PER_CHUNK) * STEP_TILES
+            return step // STEPS_PER_CHUNK, range(first, first + STEP_TILES)
 
         def transpose(step):
             chunk, tiles = tiles_of(step)
@@ -155,31 +157,21 @@ def tile_slidingcacheattention_pa_t_kernel(
             flipped_of[step] = flipped
 
         def regroup(step):
-            chunk, tiles = tiles_of(step)
-            if step % CHUNK_STEPS == 0:
-                grouped = stage.tile([P, CHUNK_TILES, P, PACK], BF16, align_bytes=64)
-                grouped_of[chunk] = grouped
-            nc.scalar.copy(
-                out=grouped_of[chunk][:, tiles[0] : tiles[0] + STEP_TILES].bitcast(F32),
-                in_=flipped_of[step][:].rearrange("p a u r -> p a r u"),
-            )
+            grouped = stage.tile([P, STEP_TILES, P, PACK], BF16, align_bytes=64)
+            nc.scalar.copy(out=grouped[:].bitcast(F32), in_=flipped_of[step][:].rearrange("p a u r -> p a r u"))
+            grouped_of[step] = grouped
 
-        def quantise(chunk):
-            x_codes = stage.tile([P, CHUNK_TOKENS], U32, align_bytes=64)
-            x_scales = stage.tile([P, CHUNK_TOKENS], U8, align_bytes=64)
+        def project(step):
+            x_codes = stage.tile([P, STEP_TILES * P], U32, align_bytes=64)
+            x_scales = stage.tile([P, STEP_TILES * P], U8, align_bytes=64)
             nc.vector.quantize_mx(
                 out=x_codes[:].bitcast(FP8X4),
                 scales=x_scales[:],
-                in_=grouped_of[chunk][:].rearrange("p t r j -> p (t r j)"),
+                in_=grouped_of[step][:].rearrange("p a r j -> p (a r j)"),
             )
-            quantised_of[chunk] = (x_codes, x_scales)
-
-        def project(step):
-            chunk, tiles = tiles_of(step)
-            x_codes, x_scales = quantised_of[chunk]
             proj_of[step] = []
-            for t in tiles:
-                tokens = slice(t * P, (t + 1) * P)
+            for a in range(STEP_TILES):
+                tokens = slice(a * P, (a + 1) * P)
                 proj = proj_pool.tile([P, FEATURES], F32)
                 nc.tensor.matmul_mx(
                     out=proj[:],
@@ -194,82 +186,83 @@ def tile_slidingcacheattention_pa_t_kernel(
 
         def norm(step):
             chunk, tiles = tiles_of(step)
-            if step % CHUNK_STEPS == 0:
-                values = stage.tile([P, CHUNK_TILES, HEAD], F32)
+            if step % STEPS_PER_CHUNK == 0:
+                values = results.tile([P, CHUNK_TILES, HEAD], F32)
                 values_of[chunk] = values
             squares = stage.tile([P, STEP_TILES, ROTATED, HEAD], BF16)
             sumsq = stats.tile([P, STEP_TILES * ROTATED], F32)
-            for a, t in enumerate(tiles):
-                proj = proj_of[step][a]
+            for a in range(STEP_TILES):
                 for h in range(ROTATED):
                     nc.scalar.activation(
                         out=squares[:, a, h, :],
-                        in_=proj[:, h * HEAD : (h + 1) * HEAD],
+                        in_=proj_of[step][a][:, h * HEAD : (h + 1) * HEAD],
                         func=ACT.Square,
                         accum_out=sumsq[:, a * ROTATED + h : a * ROTATED + h + 1],
                     )
-                nc.scalar.copy(out=values_of[chunk][:, t, :], in_=proj[:, ROTATED * HEAD : FEATURES])
-            rms = stats.tile([P, STEP_TILES * ROTATED], F32)
-            nc.scalar.activation(out=rms[:], in_=sumsq[:], func=ACT.Sqrt, scale=1.0 / HEAD, bias=eps[:])
-            rms_of[step] = rms
+            for a, t in enumerate(tiles):
+                nc.scalar.copy(out=values_of[chunk][:, t, :], in_=proj_of[step][a][:, ROTATED * HEAD : FEATURES])
+            rstd = stats.tile([P, STEP_TILES * ROTATED], F32)
+            nc.scalar.activation(
+                out=rstd[:], in_=sumsq[:], func=ACT.Abs_reciprocal_sqrt, scale=1.0 / HEAD, bias=eps[:]
+            )
+            rstd_of[step] = rstd
+
+        rotated_of = {}
 
         def rotate(step):
             chunk, tiles = tiles_of(step)
             block = chunk % BLOCKS
-            if step % CHUNK_STEPS == 0:
-                products = stage.tile([P, ROTATED, CHUNK_TILES, 2 * HEAD], F32)
-                products_of[chunk] = products
-            rstd = stats.tile([P, STEP_TILES * ROTATED], F32)
-            nc.vector.reciprocal(out=rstd[:], in_=rms_of[step][:])
+            if step % STEPS_PER_CHUNK == 0:
+                rotated = results.tile([P, ROTATED, CHUNK_TILES, HEAD], F32)
+                rotated_of[chunk] = rotated
+            first = stage.tile([P, ROTATED, STEP_TILES, HEAD], F32)
+            second = stage.tile([P, ROTATED, STEP_TILES, HEAD], F32)
+            rstd = rstd_of[step]
             for a, t in enumerate(tiles):
                 for h in range(ROTATED):
                     kind = h // 2
-                    nc.vector.scalar_tensor_tensor(
-                        out=products_of[chunk][:, h, t, :].rearrange("p (d two) -> p d two", two=2),
-                        in0=proj_of[step][a][:, h * HEAD : (h + 1) * HEAD].unsqueeze(2).to_broadcast([P, HEAD, 2]),
-                        scalar=rstd[:, a * ROTATED + h : a * ROTATED + h + 1],
-                        in1=tables[kind][:, block * CHUNK_TILES + t, :].rearrange("p (d two) -> p d two", two=2),
-                        op0=ALU.mult,
-                        op1=ALU.mult,
-                    )
-
-        def finish(chunk):
-            b, rows = chunk_rows(chunk)
-            by_pair = products_of[chunk][:].rearrange("p h t (i y two) -> p (h t i) y two", y=2, two=2)
-            rotated = stage.tile([P, ROTATED, CHUNK_TILES, HEAD], F32)
+                    pairs = proj_of[step][a][:, h * HEAD : (h + 1) * HEAD].rearrange("p (i two) -> p i two", two=2)
+                    for parity, product in enumerate((first[:, h, a, :], second[:, h, a, :])):
+                        nc.vector.scalar_tensor_tensor(
+                            out=product.rearrange("p (i two) -> p i two", two=2),
+                            in0=pairs[:, :, parity : parity + 1].to_broadcast([P, HALF, 2]),
+                            scalar=rstd[:, a * ROTATED + h : a * ROTATED + h + 1],
+                            in1=tables[kind][parity][:, block * CHUNK_TILES + t, :].rearrange("p (i two) -> p i two", two=2),
+                            op0=ALU.mult,
+                            op1=ALU.mult,
+                        )
             nc.gpsimd.tensor_tensor(
-                out=rotated[:].rearrange("p h t (i two) -> p (h t i) two", two=2),
-                in0=by_pair[:, :, 0, :],
-                in1=by_pair[:, :, 1, :],
-                op=ALU.add,
+                out=rotated_of[chunk][:, :, tiles[0] : tiles[0] + STEP_TILES, :], in0=first[:], in1=second[:], op=ALU.add
             )
+
+        def store(chunk):
+            b, rows = chunk_rows(chunk)
             nc.sync.dma_start(
                 out=out_0[b, :, rows, :].rearrange("h (p t) d -> p h (t d)", t=CHUNK_TILES),
-                in_=rotated[:, 0:2].rearrange("p h t d -> p h (t d)"),
+                in_=rotated_of[chunk][:, 0:2].rearrange("p h t d -> p h (t d)"),
             )
             nc.sync.dma_start(
                 out=out_1[b, 0, rows, :].rearrange("(p t) d -> p (t d)", t=CHUNK_TILES),
-                in_=rotated[:, 2].rearrange("p t d -> p (t d)"),
+                in_=rotated_of[chunk][:, 2].rearrange("p t d -> p (t d)"),
             )
             nc.sync.dma_start(
                 out=out_2[b, 0, rows, :].rearrange("(p t) d -> p (t d)", t=CHUNK_TILES),
                 in_=values_of[chunk][:].rearrange("p t d -> p (t d)"),
             )
 
-        for step in range(-4, STEPS):
-            if step + 4 < STEPS:
-                transpose(step + 4)
+        LEAD = 3
+        for step in range(-LEAD, STEPS):
+            if step + LEAD < BLOCKS:
+                build_tables(step + LEAD)
+            if step + 3 < STEPS:
+                transpose(step + 3)
             if 0 <= step + 2 < STEPS:
-                if (step + 2) % CHUNK_STEPS == 0:
-                    quantise((step + 2) // CHUNK_STEPS)
                 project(step + 2)
-            if (step + 4) % CHUNK_STEPS == 0 and (step + 4) // CHUNK_STEPS < BLOCKS:
-                build_tables((step + 4) // CHUNK_STEPS)
             if 0 <= step + 1 < STEPS:
                 norm(step + 1)
-            if step + 4 < STEPS:
-                regroup(step + 4)
+            if step + 3 < STEPS:
+                regroup(step + 3)
             if step >= 0:
                 rotate(step)
-                if step % CHUNK_STEPS == CHUNK_STEPS - 1:
-                    finish(step // CHUNK_STEPS)
+                if step % STEPS_PER_CHUNK == STEPS_PER_CHUNK - 1:
+                    store(step // STEPS_PER_CHUNK)

@@ -31,6 +31,8 @@ STEPS_PER_CHUNK = CHUNK_TILES // STEP_TILES
 STEPS = CHUNKS * STEPS_PER_CHUNK
 SLOTS = TOKENS // P
 
+LEAD = 8
+
 FLOPS = 2 * BATCH * TOKENS * DIM * FEATURES
 
 
@@ -55,6 +57,7 @@ def tile_slidingcacheattention_pa_t_kernel(
     with ExitStack() as stack:
         const = stack.enter_context(tc.tile_pool(name="const", bufs=1))
         resident = stack.enter_context(tc.tile_pool(name="resident", bufs=CHUNKS))
+        quantised = stack.enter_context(tc.tile_pool(name="quantised", bufs=LEAD))
         stage = stack.enter_context(tc.tile_pool(name="stage", bufs=3))
         stats = stack.enter_context(tc.tile_pool(name="stats", bufs=4))
         results = stack.enter_context(tc.tile_pool(name="results", bufs=3))
@@ -78,15 +81,15 @@ def tile_slidingcacheattention_pa_t_kernel(
 
         load_x(0)
 
+        norm_gain = const.tile([P, 2, HEAD], BF16)
+        nc.sync.dma_start(out=norm_gain[:, 0, :], in_=wq_norm.partition_broadcast(P))
+        nc.sync.dma_start(out=norm_gain[:, 1, :], in_=wk_norm.partition_broadcast(P))
         angle = const.tile([P, 3, SLOTS, HALF], BF16)
         for plane, freqs in enumerate((freqs_cos, freqs_sin, freqs_cos)):
             nc.sync.dma_start(
                 out=angle[:, plane].rearrange("p (c t) i -> p c (t i)", t=CHUNK_TILES),
                 in_=freqs.rearrange("(c p t) i -> p c (t i)", p=P, t=CHUNK_TILES),
             )
-        norm_gain = const.tile([P, 2, HEAD], BF16)
-        nc.sync.dma_start(out=norm_gain[:, 0, :], in_=wq_norm.partition_broadcast(P))
-        nc.sync.dma_start(out=norm_gain[:, 1, :], in_=wk_norm.partition_broadcast(P))
 
         weights = (
             (Wq_words, Wq_scales, 0, 2 * HEAD),
@@ -101,13 +104,14 @@ def tile_slidingcacheattention_pa_t_kernel(
             )
         w_scales = const.tile([P, FEATURES], U8, align_bytes=64)
         nc.vector.memset(w_scales[:].bitcast(I32), 0)
-        for words, scales, first, width in weights:
-            for quadrant in range(4):
+        for quadrant in range(4):
+            load_x(1 + quadrant)
+            for words, scales, first, width in weights:
                 nc.sync.dma_start(
                     out=w_scales[32 * quadrant : 32 * quadrant + 4, first : first + width].bitcast(I32),
                     in_=scales[0, 4 * quadrant : 4 * quadrant + 4, :].bitcast(I32),
                 )
-        for chunk in range(1, CHUNKS):
+        for chunk in range(5, CHUNKS):
             load_x(chunk)
 
         identity = const.tile([P, P], F32)
@@ -131,17 +135,18 @@ def tile_slidingcacheattention_pa_t_kernel(
         ]
 
         def build_tables(block):
+            builder = nc.vector if block < BLOCKS // 2 else nc.gpsimd
             slots = slice(block * CHUNK_TILES, (block + 1) * CHUNK_TILES)
             for kind in range(2):
                 for parity in range(2):
-                    nc.vector.tensor_tensor(
+                    builder.tensor_tensor(
                         out=tables[kind][parity][:, slots, :].rearrange("p s (i two) -> p s i two", two=2),
                         in0=angle[:, parity : parity + 2, slots, :].rearrange("p two s i -> p s i two"),
                         in1=gains[parity][:, kind].unsqueeze(1).to_broadcast([P, CHUNK_TILES, HALF, 2]),
                         op=ALU.mult,
                     )
 
-        flipped_of, grouped_of, proj_of, rstd_of, values_of = {}, {}, {}, {}, {}
+        flipped_of, grouped_of, quantised_of, proj_of, rstd_of, values_of = {}, {}, {}, {}, {}, {}
 
         def tiles_of(step):
             first = (step % STEPS_PER_CHUNK) * STEP_TILES
@@ -161,14 +166,18 @@ def tile_slidingcacheattention_pa_t_kernel(
             nc.scalar.copy(out=grouped[:].bitcast(F32), in_=flipped_of[step][:].rearrange("p a u r -> p a r u"))
             grouped_of[step] = grouped
 
-        def project(step):
-            x_codes = stage.tile([P, STEP_TILES * P], U32, align_bytes=64)
-            x_scales = stage.tile([P, STEP_TILES * P], U8, align_bytes=64)
+        def quantise(step):
+            x_codes = quantised.tile([P, STEP_TILES * P], U32, align_bytes=64)
+            x_scales = quantised.tile([P, STEP_TILES * P], U8, align_bytes=64)
             nc.vector.quantize_mx(
                 out=x_codes[:].bitcast(FP8X4),
                 scales=x_scales[:],
                 in_=grouped_of[step][:].rearrange("p a r j -> p (a r j)"),
             )
+            quantised_of[step] = (x_codes, x_scales)
+
+        def project(step):
+            x_codes, x_scales = quantised_of[step]
             proj_of[step] = []
             for a in range(STEP_TILES):
                 tokens = slice(a * P, (a + 1) * P)
@@ -231,7 +240,8 @@ def tile_slidingcacheattention_pa_t_kernel(
                             op0=ALU.mult,
                             op1=ALU.mult,
                         )
-            nc.gpsimd.tensor_tensor(
+            adder = nc.gpsimd if step < STEPS - 1 else nc.vector
+            adder.tensor_tensor(
                 out=rotated_of[chunk][:, :, tiles[0] : tiles[0] + STEP_TILES, :], in0=first[:], in1=second[:], op=ALU.add
             )
 
@@ -250,18 +260,21 @@ def tile_slidingcacheattention_pa_t_kernel(
                 in_=values_of[chunk][:].rearrange("p t d -> p (t d)"),
             )
 
-        LEAD = 3
-        for step in range(-LEAD, STEPS):
-            if step + LEAD < BLOCKS:
-                build_tables(step + LEAD)
-            if step + 3 < STEPS:
-                transpose(step + 3)
+        assert BLOCKS <= LEAD
+        for step in range(-LEAD - 1, STEPS):
+            ahead = step + LEAD + 1
+            if ahead < STEPS:
+                transpose(ahead)
             if 0 <= step + 2 < STEPS:
                 project(step + 2)
             if 0 <= step + 1 < STEPS:
                 norm(step + 1)
-            if step + 3 < STEPS:
-                regroup(step + 3)
+            if ahead < STEPS:
+                regroup(ahead)
+            if 0 <= ahead - 1 < STEPS:
+                quantise(ahead - 1)
+            if ahead < BLOCKS:
+                build_tables(ahead)
             if step >= 0:
                 rotate(step)
                 if step % STEPS_PER_CHUNK == STEPS_PER_CHUNK - 1:

@@ -31,8 +31,6 @@ STEPS_PER_CHUNK = CHUNK_TILES // STEP_TILES
 STEPS = CHUNKS * STEPS_PER_CHUNK
 SLOTS = TOKENS // P
 
-LEAD = 8
-
 FLOPS = 2 * BATCH * TOKENS * DIM * FEATURES
 
 
@@ -57,7 +55,6 @@ def tile_slidingcacheattention_pa_t_kernel(
     with ExitStack() as stack:
         const = stack.enter_context(tc.tile_pool(name="const", bufs=1))
         resident = stack.enter_context(tc.tile_pool(name="resident", bufs=CHUNKS))
-        quantised = stack.enter_context(tc.tile_pool(name="quantised", bufs=LEAD))
         stage = stack.enter_context(tc.tile_pool(name="stage", bufs=3))
         stats = stack.enter_context(tc.tile_pool(name="stats", bufs=4))
         results = stack.enter_context(tc.tile_pool(name="results", bufs=3))
@@ -79,17 +76,17 @@ def tile_slidingcacheattention_pa_t_kernel(
             )
             x_chunks.append(x_chunk)
 
-        load_x(0)
-
-        norm_gain = const.tile([P, 2, HEAD], BF16)
-        nc.sync.dma_start(out=norm_gain[:, 0, :], in_=wq_norm.partition_broadcast(P))
-        nc.sync.dma_start(out=norm_gain[:, 1, :], in_=wk_norm.partition_broadcast(P))
         angle = const.tile([P, 3, SLOTS, HALF], BF16)
         for plane, freqs in enumerate((freqs_cos, freqs_sin, freqs_cos)):
             nc.sync.dma_start(
                 out=angle[:, plane].rearrange("p (c t) i -> p c (t i)", t=CHUNK_TILES),
                 in_=freqs.rearrange("(c p t) i -> p c (t i)", p=P, t=CHUNK_TILES),
             )
+        norm_gain = const.tile([P, 2, HEAD], BF16)
+        nc.sync.dma_start(out=norm_gain[:, 0, :], in_=wq_norm.partition_broadcast(P))
+        nc.sync.dma_start(out=norm_gain[:, 1, :], in_=wk_norm.partition_broadcast(P))
+
+        load_x(0)
 
         weights = (
             (Wq_words, Wq_scales, 0, 2 * HEAD),
@@ -104,14 +101,13 @@ def tile_slidingcacheattention_pa_t_kernel(
             )
         w_scales = const.tile([P, FEATURES], U8, align_bytes=64)
         nc.vector.memset(w_scales[:].bitcast(I32), 0)
-        for quadrant in range(4):
-            load_x(1 + quadrant)
-            for words, scales, first, width in weights:
+        for words, scales, first, width in weights:
+            for quadrant in range(4):
                 nc.sync.dma_start(
                     out=w_scales[32 * quadrant : 32 * quadrant + 4, first : first + width].bitcast(I32),
                     in_=scales[0, 4 * quadrant : 4 * quadrant + 4, :].bitcast(I32),
                 )
-        for chunk in range(5, CHUNKS):
+        for chunk in range(1, CHUNKS):
             load_x(chunk)
 
         identity = const.tile([P, P], F32)
@@ -135,18 +131,17 @@ def tile_slidingcacheattention_pa_t_kernel(
         ]
 
         def build_tables(block):
-            builder = nc.vector if block < BLOCKS // 2 else nc.gpsimd
             slots = slice(block * CHUNK_TILES, (block + 1) * CHUNK_TILES)
             for kind in range(2):
                 for parity in range(2):
-                    builder.tensor_tensor(
+                    nc.vector.tensor_tensor(
                         out=tables[kind][parity][:, slots, :].rearrange("p s (i two) -> p s i two", two=2),
                         in0=angle[:, parity : parity + 2, slots, :].rearrange("p two s i -> p s i two"),
                         in1=gains[parity][:, kind].unsqueeze(1).to_broadcast([P, CHUNK_TILES, HALF, 2]),
                         op=ALU.mult,
                     )
 
-        flipped_of, grouped_of, quantised_of, proj_of, rstd_of, values_of = {}, {}, {}, {}, {}, {}
+        flipped_of, grouped_of, proj_of, rstd_of, values_of = {}, {}, {}, {}, {}
 
         def tiles_of(step):
             first = (step % STEPS_PER_CHUNK) * STEP_TILES
@@ -166,18 +161,14 @@ def tile_slidingcacheattention_pa_t_kernel(
             nc.scalar.copy(out=grouped[:].bitcast(F32), in_=flipped_of[step][:].rearrange("p a u r -> p a r u"))
             grouped_of[step] = grouped
 
-        def quantise(step):
-            x_codes = quantised.tile([P, STEP_TILES * P], U32, align_bytes=64)
-            x_scales = quantised.tile([P, STEP_TILES * P], U8, align_bytes=64)
+        def project(step):
+            x_codes = stage.tile([P, STEP_TILES * P], U32, align_bytes=64)
+            x_scales = stage.tile([P, STEP_TILES * P], U8, align_bytes=64)
             nc.vector.quantize_mx(
                 out=x_codes[:].bitcast(FP8X4),
                 scales=x_scales[:],
                 in_=grouped_of[step][:].rearrange("p a r j -> p (a r j)"),
             )
-            quantised_of[step] = (x_codes, x_scales)
-
-        def project(step):
-            x_codes, x_scales = quantised_of[step]
             proj_of[step] = []
             for a in range(STEP_TILES):
                 tokens = slice(a * P, (a + 1) * P)
@@ -260,21 +251,18 @@ def tile_slidingcacheattention_pa_t_kernel(
                 in_=values_of[chunk][:].rearrange("p t d -> p (t d)"),
             )
 
-        assert BLOCKS <= LEAD
-        for step in range(-LEAD - 1, STEPS):
-            ahead = step + LEAD + 1
-            if ahead < STEPS:
-                transpose(ahead)
+        LEAD = 3
+        for step in range(-LEAD, STEPS):
+            if step + 3 < STEPS:
+                transpose(step + 3)
             if 0 <= step + 2 < STEPS:
                 project(step + 2)
+            if step + LEAD < BLOCKS:
+                build_tables(step + LEAD)
             if 0 <= step + 1 < STEPS:
                 norm(step + 1)
-            if ahead < STEPS:
-                regroup(ahead)
-            if 0 <= ahead - 1 < STEPS:
-                quantise(ahead - 1)
-            if ahead < BLOCKS:
-                build_tables(ahead)
+            if step + 3 < STEPS:
+                regroup(step + 3)
             if step >= 0:
                 rotate(step)
                 if step % STEPS_PER_CHUNK == STEPS_PER_CHUNK - 1:

@@ -94,19 +94,33 @@ def tile_slidingcacheattention_pa_t_kernel(
             (Wv_words, Wv_scales, 3 * HEAD, HEAD),
         )
         w_codes = const.tile([P, FEATURES], U32, align_bytes=64)
+        w_codes_raw = const.tile([P, ROTATED * HEAD], U32)
         for words, scales, first, width in weights:
+            target = w_codes_raw if first < ROTATED * HEAD else w_codes
             nc.sync.dma_start(
-                out=w_codes[:, first : first + width].bitcast(I32),
+                out=target[:, first : first + width].bitcast(I32),
                 in_=words.rearrange("g p n t -> (g p) (n t)").bitcast(I32),
             )
         w_scales = const.tile([P, FEATURES], U8, align_bytes=64)
+        w_scales_raw = const.tile([P, ROTATED * HEAD], U8)
         nc.vector.memset(w_scales[:].bitcast(I32), 0)
+        nc.vector.memset(w_scales_raw[:].bitcast(I32), 0)
         for words, scales, first, width in weights:
+            target = w_scales_raw if first < ROTATED * HEAD else w_scales
             for quadrant in range(4):
                 nc.sync.dma_start(
-                    out=w_scales[32 * quadrant : 32 * quadrant + 4, first : first + width].bitcast(I32),
+                    out=target[32 * quadrant : 32 * quadrant + 4, first : first + width].bitcast(I32),
                     in_=scales[0, 4 * quadrant : 4 * quadrant + 4, :].bitcast(I32),
                 )
+        for parity in range(2):
+            nc.vector.tensor_copy(
+                out=w_codes[:, 0 : ROTATED * HEAD].bitcast(I32).rearrange("p (h par i) -> p h par i", par=2, i=HALF)[:, :, parity, :],
+                in_=w_codes_raw[:].bitcast(I32).rearrange("p (h i par) -> p h i par", par=2, i=HALF)[:, :, :, parity],
+            )
+            nc.vector.tensor_copy(
+                out=w_scales[:, 0 : ROTATED * HEAD].rearrange("p (h par i) -> p h par i", par=2, i=HALF)[:, :, parity, :],
+                in_=w_scales_raw[:].rearrange("p (h i par) -> p h i par", par=2, i=HALF)[:, :, :, parity],
+            )
         for chunk in range(1, CHUNKS):
             load_x(chunk)
 
@@ -125,17 +139,14 @@ def tile_slidingcacheattention_pa_t_kernel(
         nc.vector.tensor_copy(out=gain_odd[:, :, :, 1:2], in_=gain_pairs[:, :, :, 1:2])
         gains = (gain_even, gain_odd)
 
-        tables = [
-            [const.tile([P, SLOTS, HEAD], F32, name="table_%d_%d" % (kind, parity)) for parity in range(2)]
-            for kind in range(2)
-        ]
+        tables = [const.tile([P, SLOTS, 2, HEAD], F32, name="table_%d" % kind) for kind in range(2)]
 
         def build_tables(block):
             slots = slice(block * CHUNK_TILES, (block + 1) * CHUNK_TILES)
             for kind in range(2):
                 for parity in range(2):
                     nc.vector.tensor_tensor(
-                        out=tables[kind][parity][:, slots, :].rearrange("p s (i two) -> p s i two", two=2),
+                        out=tables[kind][:, slots, parity, :].rearrange("p s (i two) -> p s i two", two=2),
                         in0=angle[:, parity : parity + 2, slots, :].rearrange("p two s i -> p s i two"),
                         in1=gains[parity][:, kind].unsqueeze(1).to_broadcast([P, CHUNK_TILES, HALF, 2]),
                         op=ALU.mult,
@@ -215,25 +226,23 @@ def tile_slidingcacheattention_pa_t_kernel(
             if step % STEPS_PER_CHUNK == 0:
                 rotated = results.tile([P, ROTATED, CHUNK_TILES, HEAD], F32)
                 rotated_of[chunk] = rotated
-            first = stage.tile([P, ROTATED, STEP_TILES, HEAD], F32)
-            second = stage.tile([P, ROTATED, STEP_TILES, HEAD], F32)
+            products = stage.tile([P, 2, ROTATED, STEP_TILES, HEAD], F32)
             rstd = rstd_of[step]
             for a, t in enumerate(tiles):
                 for h in range(ROTATED):
                     kind = h // 2
-                    pairs = proj_of[step][a][:, h * HEAD : (h + 1) * HEAD].rearrange("p (i two) -> p i two", two=2)
-                    for parity, product in enumerate((first[:, h, a, :], second[:, h, a, :])):
-                        nc.vector.scalar_tensor_tensor(
-                            out=product.rearrange("p (i two) -> p i two", two=2),
-                            in0=pairs[:, :, parity : parity + 1].to_broadcast([P, HALF, 2]),
-                            scalar=rstd[:, a * ROTATED + h : a * ROTATED + h + 1],
-                            in1=tables[kind][parity][:, block * CHUNK_TILES + t, :].rearrange("p (i two) -> p i two", two=2),
-                            op0=ALU.mult,
-                            op1=ALU.mult,
-                        )
+                    head = proj_of[step][a][:, h * HEAD : (h + 1) * HEAD]
+                    nc.vector.scalar_tensor_tensor(
+                        out=products[:, :, h, a, :].rearrange("p par (i two) -> p par i two", two=2),
+                        in0=head.rearrange("p (par i) -> p par i", par=2).unsqueeze(3).to_broadcast([P, 2, HALF, 2]),
+                        scalar=rstd[:, a * ROTATED + h : a * ROTATED + h + 1],
+                        in1=tables[kind][:, block * CHUNK_TILES + t, :, :].rearrange("p par (i two) -> p par i two", two=2),
+                        op0=ALU.mult,
+                        op1=ALU.mult,
+                    )
             adder = nc.gpsimd if step < STEPS - 1 else nc.vector
             adder.tensor_tensor(
-                out=rotated_of[chunk][:, :, tiles[0] : tiles[0] + STEP_TILES, :], in0=first[:], in1=second[:], op=ALU.add
+                out=rotated_of[chunk][:, :, tiles[0] : tiles[0] + STEP_TILES, :], in0=products[:, 0], in1=products[:, 1], op=ALU.add
             )
 
         def store(chunk):

@@ -30,6 +30,7 @@ CHUNKS = BATCH * BLOCKS
 STEPS_PER_CHUNK = CHUNK_TILES // STEP_TILES
 STEPS = CHUNKS * STEPS_PER_CHUNK
 SLOTS = TOKENS // P
+PREFETCH = 5
 
 FLOPS = 2 * BATCH * TOKENS * DIM * FEATURES
 
@@ -112,16 +113,7 @@ def tile_slidingcacheattention_pa_t_kernel(
                     out=target[32 * quadrant : 32 * quadrant + 4, first : first + width].bitcast(I32),
                     in_=scales[0, 4 * quadrant : 4 * quadrant + 4, :].bitcast(I32),
                 )
-        for parity in range(2):
-            nc.vector.tensor_copy(
-                out=w_codes[:, 0 : ROTATED * HEAD].bitcast(I32).rearrange("p (h par i) -> p h par i", par=2, i=HALF)[:, :, parity, :],
-                in_=w_codes_raw[:].bitcast(I32).rearrange("p (h i par) -> p h i par", par=2, i=HALF)[:, :, :, parity],
-            )
-            nc.vector.tensor_copy(
-                out=w_scales[:, 0 : ROTATED * HEAD].rearrange("p (h par i) -> p h par i", par=2, i=HALF)[:, :, parity, :],
-                in_=w_scales_raw[:].rearrange("p (h i par) -> p h i par", par=2, i=HALF)[:, :, :, parity],
-            )
-        for chunk in range(1, CHUNKS):
+        for chunk in range(1, PREFETCH):
             load_x(chunk)
 
         identity = const.tile([P, P], F32)
@@ -151,6 +143,17 @@ def tile_slidingcacheattention_pa_t_kernel(
                         in1=gains[parity][:, kind].unsqueeze(1).to_broadcast([P, CHUNK_TILES, HALF, 2]),
                         op=ALU.mult,
                     )
+
+        def permute_weights():
+            for parity in range(2):
+                nc.vector.tensor_copy(
+                    out=w_codes[:, 0 : ROTATED * HEAD].bitcast(I32).rearrange("p (h par i) -> p h par i", par=2, i=HALF)[:, :, parity, :],
+                    in_=w_codes_raw[:].bitcast(I32).rearrange("p (h i par) -> p h i par", par=2, i=HALF)[:, :, :, parity],
+                )
+                nc.vector.tensor_copy(
+                    out=w_scales[:, 0 : ROTATED * HEAD].rearrange("p (h par i) -> p h par i", par=2, i=HALF)[:, :, parity, :],
+                    in_=w_scales_raw[:].rearrange("p (h i par) -> p h i par", par=2, i=HALF)[:, :, :, parity],
+                )
 
         flipped_of, grouped_of, proj_of, rstd_of, values_of = {}, {}, {}, {}, {}
 
@@ -240,21 +243,34 @@ def tile_slidingcacheattention_pa_t_kernel(
                         op0=ALU.mult,
                         op1=ALU.mult,
                     )
-            adder = nc.gpsimd if step < STEPS - 1 else nc.vector
-            adder.tensor_tensor(
-                out=rotated_of[chunk][:, :, tiles[0] : tiles[0] + STEP_TILES, :], in0=products[:, 0], in1=products[:, 1], op=ALU.add
+            here = slice(tiles[0], tiles[0] + STEP_TILES)
+            if step < STEPS - 1:
+                nc.gpsimd.tensor_tensor(
+                    out=rotated_of[chunk][:, :, here, :], in0=products[:, 0], in1=products[:, 1], op=ALU.add
+                )
+            else:
+                for heads in (slice(0, 2), slice(2, ROTATED)):
+                    nc.vector.tensor_tensor(
+                        out=rotated_of[chunk][:, heads, here, :],
+                        in0=products[:, 0, heads],
+                        in1=products[:, 1, heads],
+                        op=ALU.add,
+                    )
+
+        def store_rotated(chunk, first_tile, tile_count):
+            b, rows = chunk_rows(chunk)
+            here = slice(first_tile, first_tile + tile_count)
+            nc.sync.dma_start(
+                out=out_0[b, :, rows, :].rearrange("h (p t) d -> p h t d", t=CHUNK_TILES)[:, :, here, :],
+                in_=rotated_of[chunk][:, 0:2, here, :],
+            )
+            nc.sync.dma_start(
+                out=out_1[b, 0, rows, :].rearrange("(p t) d -> p t d", t=CHUNK_TILES)[:, here, :],
+                in_=rotated_of[chunk][:, 2, here, :],
             )
 
-        def store(chunk):
+        def store_values(chunk):
             b, rows = chunk_rows(chunk)
-            nc.sync.dma_start(
-                out=out_0[b, :, rows, :].rearrange("h (p t) d -> p h (t d)", t=CHUNK_TILES),
-                in_=rotated_of[chunk][:, 0:2].rearrange("p h t d -> p h (t d)"),
-            )
-            nc.sync.dma_start(
-                out=out_1[b, 0, rows, :].rearrange("(p t) d -> p (t d)", t=CHUNK_TILES),
-                in_=rotated_of[chunk][:, 2].rearrange("p t d -> p (t d)"),
-            )
             nc.sync.dma_start(
                 out=out_2[b, 0, rows, :].rearrange("(p t) d -> p (t d)", t=CHUNK_TILES),
                 in_=values_of[chunk][:].rearrange("p t d -> p (t d)"),
@@ -268,11 +284,20 @@ def tile_slidingcacheattention_pa_t_kernel(
                 project(step + 2)
             if step + LEAD < BLOCKS:
                 build_tables(step + LEAD)
+            if step + LEAD == 0:
+                permute_weights()
             if 0 <= step + 1 < STEPS:
                 norm(step + 1)
+                if (step + 1) % STEPS_PER_CHUNK == STEPS_PER_CHUNK - 1:
+                    store_values((step + 1) // STEPS_PER_CHUNK)
             if step + 3 < STEPS:
                 regroup(step + 3)
             if step >= 0:
                 rotate(step)
-                if step % STEPS_PER_CHUNK == STEPS_PER_CHUNK - 1:
-                    store(step // STEPS_PER_CHUNK)
+                chunk = step // STEPS_PER_CHUNK
+                if chunk == CHUNKS - 1:
+                    store_rotated(chunk, (step % STEPS_PER_CHUNK) * STEP_TILES, STEP_TILES)
+                elif step % STEPS_PER_CHUNK == STEPS_PER_CHUNK - 1:
+                    if chunk + PREFETCH < CHUNKS:
+                        load_x(chunk + PREFETCH)
+                    store_rotated(chunk, 0, CHUNK_TILES)

@@ -155,7 +155,7 @@ def tile_slidingcacheattention_pa_t_kernel(
                     in_=w_scales_raw[:].rearrange("p (h i par) -> p h i par", par=2, i=HALF)[:, :, :, parity],
                 )
 
-        flipped_of, grouped_of, proj_of, rstd_of, values_of = {}, {}, {}, {}, {}
+        flipped_of, grouped_of, codes_of, proj_of, rstd_of, values_of = {}, {}, {}, {}, {}, {}
 
         def tiles_of(step):
             first = (step % STEPS_PER_CHUNK) * STEP_TILES
@@ -171,21 +171,31 @@ def tile_slidingcacheattention_pa_t_kernel(
             flipped_of[step] = flipped
 
         def regroup(step):
-            grouped = stage.tile([P, STEP_TILES, P, PACK], BF16, align_bytes=64)
-            nc.scalar.copy(out=grouped[:].bitcast(F32), in_=flipped_of[step][:].rearrange("p a u r -> p a r u"))
-            grouped_of[step] = grouped
+            chunk, tiles = tiles_of(step)
+            if step % STEPS_PER_CHUNK == 0:
+                grouped = stage.tile([P, CHUNK_TILES, P, PACK], BF16, align_bytes=64)
+                grouped_of[chunk] = grouped
+            nc.scalar.copy(
+                out=grouped_of[chunk][:, tiles[0] : tiles[0] + STEP_TILES].bitcast(F32),
+                in_=flipped_of[step][:].rearrange("p a u r -> p a r u"),
+            )
 
-        def project(step):
-            x_codes = stage.tile([P, STEP_TILES * P], U32, align_bytes=64)
-            x_scales = stage.tile([P, STEP_TILES * P], U8, align_bytes=64)
+        def quantise(chunk):
+            x_codes = stage.tile([P, CHUNK_TOKENS], U32, align_bytes=64)
+            x_scales = stage.tile([P, CHUNK_TOKENS], U8, align_bytes=64)
             nc.vector.quantize_mx(
                 out=x_codes[:].bitcast(FP8X4),
                 scales=x_scales[:],
-                in_=grouped_of[step][:].rearrange("p a r j -> p (a r j)"),
+                in_=grouped_of[chunk][:].rearrange("p a r j -> p (a r j)"),
             )
+            codes_of[chunk] = (x_codes, x_scales)
+
+        def project(step):
+            chunk, tiles = tiles_of(step)
+            x_codes, x_scales = codes_of[chunk]
             proj_of[step] = []
-            for a in range(STEP_TILES):
-                tokens = slice(a * P, (a + 1) * P)
+            for t in tiles:
+                tokens = slice(t * P, (t + 1) * P)
                 proj = proj_pool.tile([P, FEATURES], F32)
                 nc.tensor.matmul_mx(
                     out=proj[:],
@@ -221,7 +231,7 @@ def tile_slidingcacheattention_pa_t_kernel(
             )
             rstd_of[step] = rstd
 
-        rotated_of = {}
+        rotated_of, products_of = {}, {}
 
         def rotate(step):
             chunk, tiles = tiles_of(step)
@@ -229,14 +239,16 @@ def tile_slidingcacheattention_pa_t_kernel(
             if step % STEPS_PER_CHUNK == 0:
                 rotated = results.tile([P, ROTATED, CHUNK_TILES, HEAD], F32)
                 rotated_of[chunk] = rotated
-            products = stage.tile([P, 2, ROTATED, STEP_TILES, HEAD], F32)
+                products = stage.tile([P, 2, ROTATED, CHUNK_TILES, HEAD], F32)
+                products_of[chunk] = products
+            products = products_of[chunk]
             rstd = rstd_of[step]
             for a, t in enumerate(tiles):
                 for h in range(ROTATED):
                     kind = h // 2
                     head = proj_of[step][a][:, h * HEAD : (h + 1) * HEAD]
                     nc.vector.scalar_tensor_tensor(
-                        out=products[:, :, h, a, :].rearrange("p par (i two) -> p par i two", two=2),
+                        out=products[:, :, h, t, :].rearrange("p par (i two) -> p par i two", two=2),
                         in0=head.rearrange("p (par i) -> p par i", par=2).unsqueeze(3).to_broadcast([P, 2, HALF, 2]),
                         scalar=rstd[:, a * ROTATED + h : a * ROTATED + h + 1],
                         in1=tables[kind][:, block * CHUNK_TILES + t, :, :].rearrange("p par (i two) -> p par i two", two=2),
@@ -244,16 +256,22 @@ def tile_slidingcacheattention_pa_t_kernel(
                         op1=ALU.mult,
                     )
             here = slice(tiles[0], tiles[0] + STEP_TILES)
-            if step < STEPS - 1:
+            if chunk < CHUNKS - 1:
+                if step % STEPS_PER_CHUNK == STEPS_PER_CHUNK - 1:
+                    nc.gpsimd.tensor_tensor(out=rotated_of[chunk][:], in0=products[:, 0], in1=products[:, 1], op=ALU.add)
+            elif step < STEPS - 1:
                 nc.gpsimd.tensor_tensor(
-                    out=rotated_of[chunk][:, :, here, :], in0=products[:, 0], in1=products[:, 1], op=ALU.add
+                    out=rotated_of[chunk][:, :, here, :],
+                    in0=products[:, 0, :, here, :],
+                    in1=products[:, 1, :, here, :],
+                    op=ALU.add,
                 )
             else:
                 for heads in (slice(0, 2), slice(2, ROTATED)):
                     nc.vector.tensor_tensor(
                         out=rotated_of[chunk][:, heads, here, :],
-                        in0=products[:, 0, heads],
-                        in1=products[:, 1, heads],
+                        in0=products[:, 0, heads, here, :],
+                        in1=products[:, 1, heads, here, :],
                         op=ALU.add,
                     )
 
@@ -276,11 +294,13 @@ def tile_slidingcacheattention_pa_t_kernel(
                 in_=values_of[chunk][:].rearrange("p t d -> p (t d)"),
             )
 
-        LEAD = 3
+        LEAD = 4
         for step in range(-LEAD, STEPS):
-            if step + 3 < STEPS:
-                transpose(step + 3)
+            if step + LEAD < STEPS:
+                transpose(step + LEAD)
             if 0 <= step + 2 < STEPS:
+                if (step + 2) % STEPS_PER_CHUNK == 0:
+                    quantise((step + 2) // STEPS_PER_CHUNK)
                 project(step + 2)
             if step + LEAD < BLOCKS:
                 build_tables(step + LEAD)
@@ -290,8 +310,8 @@ def tile_slidingcacheattention_pa_t_kernel(
                 norm(step + 1)
                 if (step + 1) % STEPS_PER_CHUNK == STEPS_PER_CHUNK - 1:
                     store_values((step + 1) // STEPS_PER_CHUNK)
-            if step + 3 < STEPS:
-                regroup(step + 3)
+            if step + LEAD < STEPS:
+                regroup(step + LEAD)
             if step >= 0:
                 rotate(step)
                 chunk = step // STEPS_PER_CHUNK

@@ -30,6 +30,9 @@ CHUNKS = BATCH * BLOCKS
 STEPS_PER_CHUNK = CHUNK_TILES // STEP_TILES
 STEPS = CHUNKS * STEPS_PER_CHUNK
 SLOTS = TOKENS // P
+VECTOR_BLOCKS = 3
+FINE_FIRST = 1
+FINE_CHUNKS = 2
 PREFETCH = 5
 
 FLOPS = 2 * BATCH * TOKENS * DIM * FEATURES
@@ -69,26 +72,45 @@ def tile_slidingcacheattention_pa_t_kernel(
 
         x_chunks = []
 
-        def load_x(chunk):
+        def load_x(chunk, queue):
             b, rows = chunk_rows(chunk)
             x_chunk = resident.tile([P, CHUNK_TILES, DIM], BF16)
-            nc.sync.dma_start(
+            queue.dma_start(
                 out=x_chunk[:], in_=x[b, rows, :].rearrange("(p t) k -> p t k", t=CHUNK_TILES)
             )
             x_chunks.append(x_chunk)
 
+        identity = const.tile([P, P], F32)
+        make_identity(nc, identity[:])
+        eps = const.tile([P, 1], F32)
+        gain_rows = const.tile([P, 2 * HEAD], BF16)
+        nc.vector.memset(gain_rows[:], 0.0)
+        signs = const.tile([P, 2, P], BF16)
+        w_scales = const.tile([P, FEATURES], U8, align_bytes=64)
+        w_scales_raw = const.tile([P, ROTATED * HEAD], U8)
+        nc.vector.memset(w_scales_raw[:].bitcast(I32), 0)
+        nc.vector.memset(w_scales[:].bitcast(I32), 0)
+        nc.vector.memset(signs[:, 0, :], -1.0)
+        nc.vector.memset(signs[:, 1, :], 1.0)
+        nc.vector.memset(eps[:], EPS)
+
+        load_x(0, nc.scalar)
+        warm = const.tile([P, 1], F32)
+        nc.scalar.activation(out=warm[:], in_=eps[:], func=ACT.Abs_reciprocal_sqrt)
+
+        nc.sync.dma_start(out=gain_rows[0:1, 0:HEAD], in_=wq_norm.unsqueeze(0))
+        nc.sync.dma_start(out=gain_rows[0:1, HEAD : 2 * HEAD], in_=wk_norm.unsqueeze(0))
         angle = const.tile([P, 3, SLOTS, HALF], BF16)
-        for plane, freqs in enumerate((freqs_cos, freqs_sin, freqs_cos)):
-            nc.sync.dma_start(
-                out=angle[:, plane].rearrange("p (c t) i -> p c (t i)", t=CHUNK_TILES),
-                in_=freqs.rearrange("(c p t) i -> p c (t i)", p=P, t=CHUNK_TILES),
-            )
-        norm_gain = const.tile([P, 2, HEAD], BF16)
-        nc.sync.dma_start(out=norm_gain[:, 0, :], in_=wq_norm.partition_broadcast(P))
-        nc.sync.dma_start(out=norm_gain[:, 1, :], in_=wk_norm.partition_broadcast(P))
 
-        load_x(0)
+        def load_angles(first_block, block_count):
+            blocks = slice(first_block, first_block + block_count)
+            for plane, freqs in enumerate((freqs_cos, freqs_sin, freqs_cos)):
+                nc.sync.dma_start(
+                    out=angle[:, plane].rearrange("p (c t) i -> p c (t i)", t=CHUNK_TILES)[:, blocks, :],
+                    in_=freqs.rearrange("(c p t) i -> p c (t i)", p=P, t=CHUNK_TILES)[:, blocks, :],
+                )
 
+        load_angles(0, 1)
         weights = (
             (Wq_words, Wq_scales, 0, 2 * HEAD),
             (Wk_words, Wk_scales, 2 * HEAD, HEAD),
@@ -102,10 +124,7 @@ def tile_slidingcacheattention_pa_t_kernel(
                 out=target[:, first : first + width].bitcast(I32),
                 in_=words.rearrange("g p n t -> (g p) (n t)").bitcast(I32),
             )
-        w_scales = const.tile([P, FEATURES], U8, align_bytes=64)
-        w_scales_raw = const.tile([P, ROTATED * HEAD], U8)
-        nc.vector.memset(w_scales[:].bitcast(I32), 0)
-        nc.vector.memset(w_scales_raw[:].bitcast(I32), 0)
+        load_angles(1, 1)
         for words, scales, first, width in weights:
             target = w_scales_raw if first < ROTATED * HEAD else w_scales
             for quadrant in range(4):
@@ -113,44 +132,47 @@ def tile_slidingcacheattention_pa_t_kernel(
                     out=target[32 * quadrant : 32 * quadrant + 4, first : first + width].bitcast(I32),
                     in_=scales[0, 4 * quadrant : 4 * quadrant + 4, :].bitcast(I32),
                 )
+        load_angles(2, BLOCKS - 2)
         for chunk in range(1, PREFETCH):
-            load_x(chunk)
+            load_x(chunk, nc.sync)
 
-        identity = const.tile([P, P], F32)
-        make_identity(nc, identity[:])
-        eps = const.tile([P, 1], F32)
-        nc.vector.memset(eps[:], EPS)
-        warm = const.tile([P, 1], F32)
-        nc.scalar.activation(out=warm[:], in_=eps[:], func=ACT.Abs_reciprocal_sqrt)
+        def spread_gains():
+            proj = proj_pool.tile([P, FEATURES], F32)
+            for sign in range(2):
+                nc.tensor.matmul(
+                    out=proj[:, sign * 2 * HEAD : (sign + 1) * 2 * HEAD],
+                    lhsT=signs[:, sign, :],
+                    rhs=gain_rows[:],
+                    start=True,
+                    stop=True,
+                )
+            return proj
 
-        gain_pairs = norm_gain[:].rearrange("p kind (i two) -> p kind i two", two=2)
-        gain_even = const.tile([P, 2, HALF, 2], F32)
-        gain_odd = const.tile([P, 2, HALF, 2], F32)
-        nc.vector.tensor_copy(out=gain_even[:], in_=gain_pairs[:, :, :, 0:1].to_broadcast([P, 2, HALF, 2]))
-        nc.vector.tensor_scalar_mul(out=gain_odd[:, :, :, 0:1], in0=gain_pairs[:, :, :, 1:2], scalar1=-1.0)
-        nc.vector.tensor_copy(out=gain_odd[:, :, :, 1:2], in_=gain_pairs[:, :, :, 1:2])
-        gains = (gain_even, gain_odd)
+        def gain_pattern(source, kind, parity):
+            by_sign = source[:].rearrange("p (sign kind i two) -> p kind two i sign", sign=2, kind=2, two=2)
+            pattern = by_sign[:, kind, 0, :, 1:2] if parity == 0 else by_sign[:, kind, 1, :, :]
+            return pattern.unsqueeze(1).to_broadcast([P, CHUNK_TILES, HALF, 2])
 
         tables = [const.tile([P, SLOTS, 2, HEAD], F32, name="table_%d" % kind) for kind in range(2)]
 
-        def build_tables(block):
+        def build_tables(block, engine, source):
             slots = slice(block * CHUNK_TILES, (block + 1) * CHUNK_TILES)
             for kind in range(2):
                 for parity in range(2):
-                    nc.vector.tensor_tensor(
+                    engine.tensor_tensor(
                         out=tables[kind][:, slots, parity, :].rearrange("p s (i two) -> p s i two", two=2),
                         in0=angle[:, parity : parity + 2, slots, :].rearrange("p two s i -> p s i two"),
-                        in1=gains[parity][:, kind].unsqueeze(1).to_broadcast([P, CHUNK_TILES, HALF, 2]),
+                        in1=gain_pattern(source, kind, parity),
                         op=ALU.mult,
                     )
 
         def permute_weights():
             for parity in range(2):
-                nc.vector.tensor_copy(
+                nc.gpsimd.tensor_copy(
                     out=w_codes[:, 0 : ROTATED * HEAD].bitcast(I32).rearrange("p (h par i) -> p h par i", par=2, i=HALF)[:, :, parity, :],
                     in_=w_codes_raw[:].bitcast(I32).rearrange("p (h i par) -> p h i par", par=2, i=HALF)[:, :, :, parity],
                 )
-                nc.vector.tensor_copy(
+                nc.gpsimd.tensor_copy(
                     out=w_scales[:, 0 : ROTATED * HEAD].rearrange("p (h par i) -> p h par i", par=2, i=HALF)[:, :, parity, :],
                     in_=w_scales_raw[:].rearrange("p (h i par) -> p h i par", par=2, i=HALF)[:, :, :, parity],
                 )
@@ -239,16 +261,23 @@ def tile_slidingcacheattention_pa_t_kernel(
             if step % STEPS_PER_CHUNK == 0:
                 rotated = results.tile([P, ROTATED, CHUNK_TILES, HEAD], F32)
                 rotated_of[chunk] = rotated
-                products = stage.tile([P, 2, ROTATED, CHUNK_TILES, HEAD], F32)
-                products_of[chunk] = products
-            products = products_of[chunk]
+            by_chunk = FINE_FIRST <= chunk < CHUNKS - FINE_CHUNKS
+            if by_chunk:
+                if step % STEPS_PER_CHUNK == 0:
+                    products = stage.tile([P, 2, ROTATED, CHUNK_TILES, HEAD], F32)
+                    products_of[chunk] = products
+                products = products_of[chunk]
+                first_slot = tiles[0]
+            else:
+                products = stage.tile([P, 2, ROTATED, STEP_TILES, HEAD], F32)
+                first_slot = 0
             rstd = rstd_of[step]
             for a, t in enumerate(tiles):
                 for h in range(ROTATED):
                     kind = h // 2
                     head = proj_of[step][a][:, h * HEAD : (h + 1) * HEAD]
                     nc.vector.scalar_tensor_tensor(
-                        out=products[:, :, h, t, :].rearrange("p par (i two) -> p par i two", two=2),
+                        out=products[:, :, h, first_slot + a, :].rearrange("p par (i two) -> p par i two", two=2),
                         in0=head.rearrange("p (par i) -> p par i", par=2).unsqueeze(3).to_broadcast([P, 2, HALF, 2]),
                         scalar=rstd[:, a * ROTATED + h : a * ROTATED + h + 1],
                         in1=tables[kind][:, block * CHUNK_TILES + t, :, :].rearrange("p par (i two) -> p par i two", two=2),
@@ -256,22 +285,19 @@ def tile_slidingcacheattention_pa_t_kernel(
                         op1=ALU.mult,
                     )
             here = slice(tiles[0], tiles[0] + STEP_TILES)
-            if chunk < CHUNKS - 1:
+            if by_chunk:
                 if step % STEPS_PER_CHUNK == STEPS_PER_CHUNK - 1:
                     nc.gpsimd.tensor_tensor(out=rotated_of[chunk][:], in0=products[:, 0], in1=products[:, 1], op=ALU.add)
             elif step < STEPS - 1:
                 nc.gpsimd.tensor_tensor(
-                    out=rotated_of[chunk][:, :, here, :],
-                    in0=products[:, 0, :, here, :],
-                    in1=products[:, 1, :, here, :],
-                    op=ALU.add,
+                    out=rotated_of[chunk][:, :, here, :], in0=products[:, 0], in1=products[:, 1], op=ALU.add
                 )
             else:
                 for heads in (slice(0, 2), slice(2, ROTATED)):
                     nc.vector.tensor_tensor(
                         out=rotated_of[chunk][:, heads, here, :],
-                        in0=products[:, 0, heads, here, :],
-                        in1=products[:, 1, heads, here, :],
+                        in0=products[:, 0, heads],
+                        in1=products[:, 1, heads],
                         op=ALU.add,
                     )
 
@@ -295,29 +321,48 @@ def tile_slidingcacheattention_pa_t_kernel(
             )
 
         LEAD = 4
-        for step in range(-LEAD, STEPS):
+        gain_bank = spread_gains()
+        transpose(0)
+        transpose(1)
+        build_tables(0, nc.vector, gain_bank)
+        regroup(0)
+        regroup(1)
+        quantise(0)
+        gain_copy = const.tile([P, FEATURES], F32)
+        nc.scalar.copy(out=gain_copy[:], in_=spread_gains()[:])
+        permute_weights()
+        project(0)
+        project(1)
+        for block in range(1, VECTOR_BLOCKS):
+            build_tables(block, nc.vector, gain_bank)
+        for block in range(VECTOR_BLOCKS, BLOCKS):
+            build_tables(block, nc.gpsimd, gain_copy)
+        norm(0)
+        transpose(2)
+        transpose(3)
+        regroup(2)
+        regroup(3)
+        for step in range(STEPS):
+            chunk = step // STEPS_PER_CHUNK
             if step + LEAD < STEPS:
                 transpose(step + LEAD)
-            if 0 <= step + 2 < STEPS:
-                if (step + 2) % STEPS_PER_CHUNK == 0:
-                    quantise((step + 2) // STEPS_PER_CHUNK)
+            if step == 0:
+                rotate(step)
+            if step + 2 < STEPS:
+                if step % STEPS_PER_CHUNK == 0:
+                    quantise(chunk + 1)
                 project(step + 2)
-            if step + LEAD < BLOCKS:
-                build_tables(step + LEAD)
-            if step + LEAD == 0:
-                permute_weights()
-            if 0 <= step + 1 < STEPS:
+            if step + 1 < STEPS:
                 norm(step + 1)
                 if (step + 1) % STEPS_PER_CHUNK == STEPS_PER_CHUNK - 1:
                     store_values((step + 1) // STEPS_PER_CHUNK)
             if step + LEAD < STEPS:
                 regroup(step + LEAD)
-            if step >= 0:
+            if step > 0:
                 rotate(step)
-                chunk = step // STEPS_PER_CHUNK
-                if chunk == CHUNKS - 1:
-                    store_rotated(chunk, (step % STEPS_PER_CHUNK) * STEP_TILES, STEP_TILES)
-                elif step % STEPS_PER_CHUNK == STEPS_PER_CHUNK - 1:
-                    if chunk + PREFETCH < CHUNKS:
-                        load_x(chunk + PREFETCH)
-                    store_rotated(chunk, 0, CHUNK_TILES)
+            if chunk == CHUNKS - 1:
+                store_rotated(chunk, (step % STEPS_PER_CHUNK) * STEP_TILES, STEP_TILES)
+            elif step % STEPS_PER_CHUNK == STEPS_PER_CHUNK - 1:
+                if chunk + PREFETCH < CHUNKS:
+                    load_x(chunk + PREFETCH, nc.sync)
+                store_rotated(chunk, 0, CHUNK_TILES)

@@ -67,8 +67,8 @@ def tile_slidingcacheattention_pa_t_kernel(
         stack.enter_context(tc.manual_schedule())
 
         def chunk_rows(chunk):
-            block = chunk % BLOCKS
-            return chunk // BLOCKS, slice(block * CHUNK_TOKENS, (block + 1) * CHUNK_TOKENS)
+            block, b = divmod(chunk, BATCH)
+            return b, slice(block * CHUNK_TOKENS, (block + 1) * CHUNK_TOKENS)
 
         x_chunks = []
 
@@ -257,7 +257,7 @@ def tile_slidingcacheattention_pa_t_kernel(
 
         def rotate(step):
             chunk, tiles = tiles_of(step)
-            block = chunk % BLOCKS
+            block = chunk // BATCH
             if step % STEPS_PER_CHUNK == 0:
                 rotated = results.tile([P, ROTATED, CHUNK_TILES, HEAD], F32)
                 rotated_of[chunk] = rotated

@@ -33,7 +33,7 @@ SLOTS = TOKENS // P
 VECTOR_BLOCKS = 3
 FINE_FIRST = 1
 FINE_CHUNKS = 2
-PREFETCH = 5
+PREFETCH = 7
 
 FLOPS = 2 * BATCH * TOKENS * DIM * FEATURES
 
@@ -102,15 +102,16 @@ def tile_slidingcacheattention_pa_t_kernel(
         nc.sync.dma_start(out=gain_rows[0:1, HEAD : 2 * HEAD], in_=wk_norm.unsqueeze(0))
         angle = const.tile([P, 3, SLOTS, HALF], BF16)
 
-        def load_angles(first_block, block_count):
-            blocks = slice(first_block, first_block + block_count)
-            for plane, freqs in enumerate((freqs_cos, freqs_sin, freqs_cos)):
+        def load_angles(block):
+            for freqs, planes in ((freqs_cos, slice(0, 3, 2)), (freqs_sin, slice(1, 2))):
+                source = freqs.rearrange("(c p t) i -> c p (t i)", p=P, t=CHUNK_TILES)[block]
+                copies = len(range(3)[planes])
                 nc.sync.dma_start(
-                    out=angle[:, plane].rearrange("p (c t) i -> p c (t i)", t=CHUNK_TILES)[:, blocks, :],
-                    in_=freqs.rearrange("(c p t) i -> p c (t i)", p=P, t=CHUNK_TILES)[:, blocks, :],
+                    out=angle[:, planes].rearrange("p q (c t) i -> p q c (t i)", t=CHUNK_TILES)[:, :, block, :],
+                    in_=source.unsqueeze(1).to_broadcast([P, copies, CHUNK_TILES * HALF]),
                 )
 
-        load_angles(0, 1)
+        load_angles(0)
         weights = (
             (Wq_words, Wq_scales, 0, 2 * HEAD),
             (Wk_words, Wk_scales, 2 * HEAD, HEAD),
@@ -124,7 +125,7 @@ def tile_slidingcacheattention_pa_t_kernel(
                 out=target[:, first : first + width].bitcast(I32),
                 in_=words.rearrange("g p n t -> (g p) (n t)").bitcast(I32),
             )
-        load_angles(1, 1)
+        load_angles(1)
         for words, scales, first, width in weights:
             target = w_scales_raw if first < ROTATED * HEAD else w_scales
             for quadrant in range(4):
@@ -132,8 +133,10 @@ def tile_slidingcacheattention_pa_t_kernel(
                     out=target[32 * quadrant : 32 * quadrant + 4, first : first + width].bitcast(I32),
                     in_=scales[0, 4 * quadrant : 4 * quadrant + 4, :].bitcast(I32),
                 )
-        load_angles(2, BLOCKS - 2)
-        for chunk in range(1, PREFETCH):
+        load_angles(2)
+        load_angles(3)
+        load_x(1, nc.sync)
+        for chunk in range(2, PREFETCH):
             load_x(chunk, nc.sync)
 
         def spread_gains():
@@ -167,15 +170,14 @@ def tile_slidingcacheattention_pa_t_kernel(
                     )
 
         def permute_weights():
-            for parity in range(2):
-                nc.gpsimd.tensor_copy(
-                    out=w_codes[:, 0 : ROTATED * HEAD].bitcast(I32).rearrange("p (h par i) -> p h par i", par=2, i=HALF)[:, :, parity, :],
-                    in_=w_codes_raw[:].bitcast(I32).rearrange("p (h i par) -> p h i par", par=2, i=HALF)[:, :, :, parity],
-                )
-                nc.gpsimd.tensor_copy(
-                    out=w_scales[:, 0 : ROTATED * HEAD].rearrange("p (h par i) -> p h par i", par=2, i=HALF)[:, :, parity, :],
-                    in_=w_scales_raw[:].rearrange("p (h i par) -> p h i par", par=2, i=HALF)[:, :, :, parity],
-                )
+            nc.gpsimd.tensor_copy(
+                out=w_codes[:, 0 : ROTATED * HEAD].bitcast(I32).rearrange("p (h par i) -> p h par i", par=2, i=HALF),
+                in_=w_codes_raw[:].bitcast(I32).rearrange("p (h i par) -> p h par i", par=2, i=HALF),
+            )
+            nc.gpsimd.tensor_copy(
+                out=w_scales[:, 0 : ROTATED * HEAD].rearrange("p (h par i) -> p h par i", par=2, i=HALF),
+                in_=w_scales_raw[:].rearrange("p (h i par) -> p h par i", par=2, i=HALF),
+            )
 
         flipped_of, grouped_of, codes_of, proj_of, rstd_of, values_of = {}, {}, {}, {}, {}, {}
 
@@ -288,18 +290,23 @@ def tile_slidingcacheattention_pa_t_kernel(
             if by_chunk:
                 if step % STEPS_PER_CHUNK == STEPS_PER_CHUNK - 1:
                     nc.gpsimd.tensor_tensor(out=rotated_of[chunk][:], in0=products[:, 0], in1=products[:, 1], op=ALU.add)
-            elif step < STEPS - 1:
+            elif chunk < CHUNKS - 1:
                 nc.gpsimd.tensor_tensor(
                     out=rotated_of[chunk][:, :, here, :], in0=products[:, 0], in1=products[:, 1], op=ALU.add
                 )
             else:
-                for heads in (slice(0, 2), slice(2, ROTATED)):
-                    nc.vector.tensor_tensor(
-                        out=rotated_of[chunk][:, heads, here, :],
-                        in0=products[:, 0, heads],
-                        in1=products[:, 1, heads],
-                        op=ALU.add,
-                    )
+                products_of[step] = products
+
+        def sum_last(step):
+            chunk, tiles = tiles_of(step)
+            here = slice(tiles[0], tiles[0] + STEP_TILES)
+            for heads in (slice(0, 2), slice(2, ROTATED)):
+                nc.vector.tensor_tensor(
+                    out=rotated_of[chunk][:, heads, here, :],
+                    in0=products_of[step][:, 0, heads],
+                    in1=products_of[step][:, 1, heads],
+                    op=ALU.add,
+                )
 
         def store_rotated(chunk, first_tile, tile_count):
             b, rows = chunk_rows(chunk)
@@ -320,7 +327,7 @@ def tile_slidingcacheattention_pa_t_kernel(
                 in_=values_of[chunk][:].rearrange("p t d -> p (t d)"),
             )
 
-        LEAD = 4
+        LEAD, RAMP, EXTRA = 4, 1, 2
         gain_bank = spread_gains()
         transpose(0)
         transpose(1)
@@ -342,10 +349,13 @@ def tile_slidingcacheattention_pa_t_kernel(
         transpose(3)
         regroup(2)
         regroup(3)
+        prepared = LEAD
         for step in range(STEPS):
             chunk = step // STEPS_PER_CHUNK
-            if step + LEAD < STEPS:
-                transpose(step + LEAD)
+            ahead = range(prepared, min(step + LEAD + min(step // RAMP, EXTRA) + 1, STEPS))
+            prepared += len(ahead)
+            for later in ahead:
+                transpose(later)
             if step == 0:
                 rotate(step)
             if step + 2 < STEPS:
@@ -356,13 +366,17 @@ def tile_slidingcacheattention_pa_t_kernel(
                 norm(step + 1)
                 if (step + 1) % STEPS_PER_CHUNK == STEPS_PER_CHUNK - 1:
                     store_values((step + 1) // STEPS_PER_CHUNK)
-            if step + LEAD < STEPS:
-                regroup(step + LEAD)
+            for later in ahead:
+                regroup(later)
             if step > 0:
                 rotate(step)
-            if chunk == CHUNKS - 1:
+            if step == STEPS - 1:
+                for last in range(STEPS - STEPS_PER_CHUNK, STEPS):
+                    sum_last(last)
+                    store_rotated(chunk, (last % STEPS_PER_CHUNK) * STEP_TILES, STEP_TILES)
+            elif CHUNKS - FINE_CHUNKS <= chunk < CHUNKS - 1:
                 store_rotated(chunk, (step % STEPS_PER_CHUNK) * STEP_TILES, STEP_TILES)
-            elif step % STEPS_PER_CHUNK == STEPS_PER_CHUNK - 1:
+            elif chunk < CHUNKS - 1 and step % STEPS_PER_CHUNK == STEPS_PER_CHUNK - 1:
                 if chunk + PREFETCH < CHUNKS:
                     load_x(chunk + PREFETCH, nc.sync)
                 store_rotated(chunk, 0, CHUNK_TILES)

from contextlib import ExitStack

import concourse.mybir as mybir
from concourse.masks import make_identity

F32 = mybir.dt.float32
BF16 = mybir.dt.bfloat16
I32 = mybir.dt.int32
U32 = mybir.dt.uint32
U8 = mybir.dt.uint8
FP8X4 = mybir.dt.float8_e4m3fn_x4
ACT = mybir.ActivationFunctionType
ALU = mybir.AluOpType

P = 128
PACK = 4
BATCH, TOKENS, DIM = 4, 2048, 512
HEAD = 128
HALF = HEAD // 2
EPS = 1e-6
ROTATED = 3
FEATURES = 4 * HEAD
WORDS = DIM // 2

CHUNK_TILES = 4
STEP_TILES = 2
CHUNK_TOKENS = CHUNK_TILES * P
BLOCKS = TOKENS // CHUNK_TOKENS
CHUNKS = BATCH * BLOCKS
STEPS_PER_CHUNK = CHUNK_TILES // STEP_TILES
STEPS = CHUNKS * STEPS_PER_CHUNK
SLOTS = TOKENS // P
VECTOR_BLOCKS = 3
FINE_FIRST = 1
FINE_CHUNKS = 2
PREFETCH = 7

FLOPS = 2 * BATCH * TOKENS * DIM * FEATURES


def tile_slidingcacheattention_pa_t_kernel(
    tc,
    x,
    freqs_cos,
    freqs_sin,
    Wq_words,
    Wq_scales,
    Wk_words,
    Wk_scales,
    Wv_words,
    Wv_scales,
    wq_norm,
    wk_norm,
    out_0,
    out_1,
    out_2,
):
    nc = tc.nc
    with ExitStack() as stack:
        const = stack.enter_context(tc.tile_pool(name="const", bufs=1))
        resident = stack.enter_context(tc.tile_pool(name="resident", bufs=CHUNKS))
        stage = stack.enter_context(tc.tile_pool(name="stage", bufs=3))
        stats = stack.enter_context(tc.tile_pool(name="stats", bufs=4))
        results = stack.enter_context(tc.tile_pool(name="results", bufs=3))
        flipped_pool = stack.enter_context(tc.psum_pool(name="flipped_pool", bufs=2))
        proj_pool = stack.enter_context(tc.psum_pool(name="proj_pool", bufs=3 * STEP_TILES))
        stack.enter_context(tc.manual_schedule())

        def chunk_rows(chunk):
            block, b = divmod(chunk, BATCH)
            return b, slice(block * CHUNK_TOKENS, (block + 1) * CHUNK_TOKENS)

        x_chunks = []

        def load_x(chunk, queue):
            b, rows = chunk_rows(chunk)
            x_chunk = resident.tile([P, CHUNK_TILES, DIM], BF16)
            queue.dma_start(
                out=x_chunk[:], in_=x[b, rows, :].rearrange("(p t) k -> p t k", t=CHUNK_TILES)
            )
            x_chunks.append(x_chunk)

        identity = const.tile([P, P], F32)
        make_identity(nc, identity[:])
        eps = const.tile([P, 1], F32)
        gain_rows = const.tile([P, 2 * HEAD], BF16)
        nc.vector.memset(gain_rows[:], 0.0)
        signs = const.tile([P, 2, P], BF16)
        w_scales = const.tile([P, FEATURES], U8, align_bytes=64)
        w_scales_raw = const.tile([P, ROTATED * HEAD], U8)
        nc.vector.memset(w_scales_raw[:].bitcast(I32), 0)
        nc.vector.memset(w_scales[:].bitcast(I32), 0)
        nc.vector.memset(signs[:, 0, :], -1.0)
        nc.vector.memset(signs[:, 1, :], 1.0)
        nc.vector.memset(eps[:], EPS)

        load_x(0, nc.scalar)
        warm = const.tile([P, 1], F32)
        nc.scalar.activation(out=warm[:], in_=eps[:], func=ACT.Abs_reciprocal_sqrt)

        nc.sync.dma_start(out=gain_rows[0:1, 0:HEAD], in_=wq_norm.unsqueeze(0))
        nc.sync.dma_start(out=gain_rows[0:1, HEAD : 2 * HEAD], in_=wk_norm.unsqueeze(0))
        angle = const.tile([P, 3, SLOTS, HALF], BF16)

        def load_angles(block):
            for freqs, planes in ((freqs_cos, slice(0, 3, 2)), (freqs_sin, slice(1, 2))):
                source = freqs.rearrange("(c p t) i -> c p (t i)", p=P, t=CHUNK_TILES)[block]
                copies = len(range(3)[planes])
                nc.sync.dma_start(
                    out=angle[:, planes].rearrange("p q (c t) i -> p q c (t i)", t=CHUNK_TILES)[:, :, block, :],
                    in_=source.unsqueeze(1).to_broadcast([P, copies, CHUNK_TILES * HALF]),
                )

        load_angles(0)
        weights = (
            (Wq_words, Wq_scales, 0, 2 * HEAD),
            (Wk_words, Wk_scales, 2 * HEAD, HEAD),
            (Wv_words, Wv_scales, 3 * HEAD, HEAD),
        )
        w_codes = const.tile([P, FEATURES], U32, align_bytes=64)
        w_codes_raw = const.tile([P, ROTATED * HEAD], U32)
        for words, scales, first, width in weights:
            target = w_codes_raw if first < ROTATED * HEAD else w_codes
            nc.sync.dma_start(
                out=target[:, first : first + width].bitcast(I32),
                in_=words.rearrange("g p n t -> (g p) (n t)").bitcast(I32),
            )
        load_angles(1)
        for words, scales, first, width in weights:
            target = w_scales_raw if first < ROTATED * HEAD else w_scales
            for quadrant in range(4):
                nc.sync.dma_start(
                    out=target[32 * quadrant : 32 * quadrant + 4, first : first + width].bitcast(I32),
                    in_=scales[0, 4 * quadrant : 4 * quadrant + 4, :].bitcast(I32),
                )
        load_angles(2)
        load_angles(3)
        load_x(1, nc.sync)
        for chunk in range(2, PREFETCH):
            load_x(chunk, nc.sync)

        def spread_gains():
            proj = proj_pool.tile([P, FEATURES], F32)
            for sign in range(2):
                nc.tensor.matmul(
                    out=proj[:, sign * 2 * HEAD : (sign + 1) * 2 * HEAD],
                    lhsT=signs[:, sign, :],
                    rhs=gain_rows[:],
                    start=True,
                    stop=True,
                )
            return proj

        def gain_pattern(source, kind, parity):
            by_sign = source[:].rearrange("p (sign kind i two) -> p kind two i sign", sign=2, kind=2, two=2)
            pattern = by_sign[:, kind, 0, :, 1:2] if parity == 0 else by_sign[:, kind, 1, :, :]
            return pattern.unsqueeze(1).to_broadcast([P, CHUNK_TILES, HALF, 2])

        tables = [const.tile([P, SLOTS, 2, HEAD], F32, name="table_%d" % kind) for kind in range(2)]

        def build_tables(block, engine, source):
            slots = slice(block * CHUNK_TILES, (block + 1) * CHUNK_TILES)
            for kind in range(2):
                for parity in range(2):
                    engine.tensor_tensor(
                        out=tables[kind][:, slots, parity, :].rearrange("p s (i two) -> p s i two", two=2),
                        in0=angle[:, parity : parity + 2, slots, :].rearrange("p two s i -> p s i two"),
                        in1=gain_pattern(source, kind, parity),
                        op=ALU.mult,
                    )

        def permute_weights():
            nc.gpsimd.tensor_copy(
                out=w_codes[:, 0 : ROTATED * HEAD].bitcast(I32).rearrange("p (h par i) -> p h par i", par=2, i=HALF),
                in_=w_codes_raw[:].bitcast(I32).rearrange("p (h i par) -> p h par i", par=2, i=HALF),
            )
            nc.gpsimd.tensor_copy(
                out=w_scales[:, 0 : ROTATED * HEAD].rearrange("p (h par i) -> p h par i", par=2, i=HALF),
                in_=w_scales_raw[:].rearrange("p (h i par) -> p h par i", par=2, i=HALF),
            )

        flipped_of, grouped_of, codes_of, proj_of, rstd_of, values_of = {}, {}, {}, {}, {}, {}

        def tiles_of(step):
            first = (step % STEPS_PER_CHUNK) * STEP_TILES
            return step // STEPS_PER_CHUNK, range(first, first + STEP_TILES)

        def transpose(step):
            chunk, tiles = tiles_of(step)
            flipped = flipped_pool.tile([P, STEP_TILES, 2, P], F32)
            for a, t in enumerate(tiles):
                words = x_chunks[chunk][:, t, :].bitcast(F32)
                for u in range(2):
                    nc.tensor.transpose(flipped[:, a, u, :], words[:, u:WORDS:2], identity[:])
            flipped_of[step] = flipped

        def regroup(step):
            chunk, tiles = tiles_of(step)
            if step % STEPS_PER_CHUNK == 0:
                grouped = stage.tile([P, CHUNK_TILES, P, PACK], BF16, align_bytes=64)
                grouped_of[chunk] = grouped
            nc.scalar.copy(
                out=grouped_of[chunk][:, tiles[0] : tiles[0] + STEP_TILES].bitcast(F32),
                in_=flipped_of[step][:].rearrange("p a u r -> p a r u"),
            )

        def quantise(chunk):
            x_codes = stage.tile([P, CHUNK_TOKENS], U32, align_bytes=64)
            x_scales = stage.tile([P, CHUNK_TOKENS], U8, align_bytes=64)
            nc.vector.quantize_mx(
                out=x_codes[:].bitcast(FP8X4),
                scales=x_scales[:],
                in_=grouped_of[chunk][:].rearrange("p a r j -> p (a r j)"),
            )
            codes_of[chunk] = (x_codes, x_scales)

        def project(step):
            chunk, tiles = tiles_of(step)
            x_codes, x_scales = codes_of[chunk]
            proj_of[step] = []
            for t in tiles:
                tokens = slice(t * P, (t + 1) * P)
                proj = proj_pool.tile([P, FEATURES], F32)
                nc.tensor.matmul_mx(
                    out=proj[:],
                    lhsT=x_codes[:, tokens].bitcast(FP8X4),
                    lhsT_scale=x_scales[:, tokens],
                    rhs=w_codes[:].bitcast(FP8X4),
                    rhs_scale=w_scales[:],
                    start=True,
                    stop=True,
                )
                proj_of[step].append(proj)

        def norm(step):
            chunk, tiles = tiles_of(step)
            if step % STEPS_PER_CHUNK == 0:
                values = results.tile([P, CHUNK_TILES, HEAD], F32)
                values_of[chunk] = values
            squares = stage.tile([P, STEP_TILES, ROTATED, HEAD], BF16)
            sumsq = stats.tile([P, STEP_TILES * ROTATED], F32)
            for a in range(STEP_TILES):
                for h in range(ROTATED):
                    nc.scalar.activation(
                        out=squares[:, a, h, :],
                        in_=proj_of[step][a][:, h * HEAD : (h + 1) * HEAD],
                        func=ACT.Square,
                        accum_out=sumsq[:, a * ROTATED + h : a * ROTATED + h + 1],
                    )
            for a, t in enumerate(tiles):
                nc.scalar.copy(out=values_of[chunk][:, t, :], in_=proj_of[step][a][:, ROTATED * HEAD : FEATURES])
            rstd = stats.tile([P, STEP_TILES * ROTATED], F32)
            nc.scalar.activation(
                out=rstd[:], in_=sumsq[:], func=ACT.Abs_reciprocal_sqrt, scale=1.0 / HEAD, bias=eps[:]
            )
            rstd_of[step] = rstd

        rotated_of, products_of = {}, {}

        def rotate(step):
            chunk, tiles = tiles_of(step)
            block = chunk // BATCH
            if step % STEPS_PER_CHUNK == 0:
                rotated = results.tile([P, ROTATED, CHUNK_TILES, HEAD], F32)
                rotated_of[chunk] = rotated
            by_chunk = FINE_FIRST <= chunk < CHUNKS - FINE_CHUNKS
            if by_chunk:
                if step % STEPS_PER_CHUNK == 0:
                    products = stage.tile([P, 2, ROTATED, CHUNK_TILES, HEAD], F32)
                    products_of[chunk] = products
                products = products_of[chunk]
                first_slot = tiles[0]
            else:
                products = stage.tile([P, 2, ROTATED, STEP_TILES, HEAD], F32)
                first_slot = 0
            rstd = rstd_of[step]
            for a, t in enumerate(tiles):
                for h in range(ROTATED):
                    kind = h // 2
                    head = proj_of[step][a][:, h * HEAD : (h + 1) * HEAD]
                    nc.vector.scalar_tensor_tensor(
                        out=products[:, :, h, first_slot + a, :].rearrange("p par (i two) -> p par i two", two=2),
                        in0=head.rearrange("p (par i) -> p par i", par=2).unsqueeze(3).to_broadcast([P, 2, HALF, 2]),
                        scalar=rstd[:, a * ROTATED + h : a * ROTATED + h + 1],
                        in1=tables[kind][:, block * CHUNK_TILES + t, :, :].rearrange("p par (i two) -> p par i two", two=2),
                        op0=ALU.mult,
                        op1=ALU.mult,
                    )
            here = slice(tiles[0], tiles[0] + STEP_TILES)
            if by_chunk:
                if step % STEPS_PER_CHUNK == STEPS_PER_CHUNK - 1:
                    nc.gpsimd.tensor_tensor(out=rotated_of[chunk][:], in0=products[:, 0], in1=products[:, 1], op=ALU.add)
            elif chunk < CHUNKS - 1:
                nc.gpsimd.tensor_tensor(
                    out=rotated_of[chunk][:, :, here, :], in0=products[:, 0], in1=products[:, 1], op=ALU.add
                )
            else:
                products_of[step] = products

        def sum_last(step):
            chunk, tiles = tiles_of(step)
            here = slice(tiles[0], tiles[0] + STEP_TILES)
            for heads in (slice(0, 2), slice(2, ROTATED)):
                nc.vector.tensor_tensor(
                    out=rotated_of[chunk][:, heads, here, :],
                    in0=products_of[step][:, 0, heads],
                    in1=products_of[step][:, 1, heads],
                    op=ALU.add,
                )

        def store_rotated(chunk, first_tile, tile_count):
            b, rows = chunk_rows(chunk)
            here = slice(first_tile, first_tile + tile_count)
            nc.sync.dma_start(
                out=out_0[b, :, rows, :].rearrange("h (p t) d -> p h t d", t=CHUNK_TILES)[:, :, here, :],
                in_=rotated_of[chunk][:, 0:2, here, :],
            )
            nc.sync.dma_start(
                out=out_1[b, 0, rows, :].rearrange("(p t) d -> p t d", t=CHUNK_TILES)[:, here, :],
                in_=rotated_of[chunk][:, 2, here, :],
            )

        def store_values(chunk):
            b, rows = chunk_rows(chunk)
            nc.sync.dma_start(
                out=out_2[b, 0, rows, :].rearrange("(p t) d -> p (t d)", t=CHUNK_TILES),
                in_=values_of[chunk][:].rearrange("p t d -> p (t d)"),
            )

        LEAD, RAMP, EXTRA = 4, 1, 2
        gain_bank = spread_gains()
        transpose(0)
        transpose(1)
        build_tables(0, nc.vector, gain_bank)
        regroup(0)
        regroup(1)
        quantise(0)
        gain_copy = const.tile([P, FEATURES], F32)
        nc.scalar.copy(out=gain_copy[:], in_=spread_gains()[:])
        permute_weights()
        project(0)
        project(1)
        for block in range(1, VECTOR_BLOCKS):
            build_tables(block, nc.vector, gain_bank)
        for block in range(VECTOR_BLOCKS, BLOCKS):
            build_tables(block, nc.gpsimd, gain_copy)
        norm(0)
        transpose(2)
        transpose(3)
        regroup(2)
        regroup(3)
        prepared = LEAD
        for step in range(STEPS):
            chunk = step // STEPS_PER_CHUNK
            ahead = range(prepared, min(step + LEAD + min(step // RAMP, EXTRA) + 1, STEPS))
            prepared += len(ahead)
            for later in ahead:
                transpose(later)
            if step == 0:
                rotate(step)
            if step + 2 < STEPS:
                if step % STEPS_PER_CHUNK == 0:
                    quantise(chunk + 1)
                project(step + 2)
            if step + 1 < STEPS:
                norm(step + 1)
                if (step + 1) % STEPS_PER_CHUNK == STEPS_PER_CHUNK - 1:
                    store_values((step + 1) // STEPS_PER_CHUNK)
            for later in ahead:
                regroup(later)
            if step > 0:
                rotate(step)
            if step == STEPS - 1:
                for last in range(STEPS - STEPS_PER_CHUNK, STEPS):
                    sum_last(last)
                    store_rotated(chunk, (last % STEPS_PER_CHUNK) * STEP_TILES, STEP_TILES)
            elif CHUNKS - FINE_CHUNKS <= chunk < CHUNKS - 1:
                store_rotated(chunk, (step % STEPS_PER_CHUNK) * STEP_TILES, STEP_TILES)
            elif chunk < CHUNKS - 1 and step % STEPS_PER_CHUNK == STEPS_PER_CHUNK - 1:
                if chunk + PREFETCH < CHUNKS:
                    load_x(chunk + PREFETCH, nc.sync)
                store_rotated(chunk, 0, CHUNK_TILES)
